import numpy as np
import ml_dtypes


def mxq(x, axis, fmt="e4m3"):
    dtype, down = {"e4m3": (ml_dtypes.float8_e4m3fn, 7), "e5m2": (ml_dtypes.float8_e5m2, 14)}[fmt]
    v = np.moveaxis(np.asarray(x, np.float32).astype(ml_dtypes.bfloat16).astype(np.float64), axis, -1)
    blocks = v.reshape(v.shape[:-1] + (-1, 32))
    amax = np.abs(blocks).max(-1, keepdims=True)
    byte = np.maximum(np.where(amax > 0, np.frexp(amax)[1] - 1 + 127, 0) - down, 1)
    scale = np.exp2(byte - 127.0)
    codes = (blocks / scale).astype(np.float32).astype(dtype).astype(np.float64)
    return np.moveaxis((codes * scale).reshape(v.shape), -1, axis)


WIDE = False


def mx_kscale(k):
    if not WIDE:
        return np.ones(k)
    levels = np.array([10, -10, 5, -5, 0])
    a = np.random.permutation(np.resize(levels, k // 512 * 4)).reshape(k // 512, 4)
    idx = np.arange(k)
    return np.exp2(a[idx // 512, idx % 128 // 32])


BF16 = ml_dtypes.bfloat16


def bf(x):
    return np.asarray(x, np.float32).astype(BF16)


def f64(x):
    return np.asarray(x).astype(np.float64)


E2M1 = np.array([0.0, 0.5, 1.0, 1.5, 2.0, 3.0, 4.0, 6.0, -0.0, -0.5, -1.0, -1.5, -2.0, -3.0, -4.0, -6.0])


def pack_weight(w, fmt):
    k, n = w.shape
    w = f64(bf(w)).reshape(k // 32, 32, n)
    amax = np.abs(w).max(1)
    if fmt == "e4m3":
        byte = np.frexp(amax)[1] - 1 + 127 - 7
    else:
        mant, ex = np.frexp(amax / 6.0)
        byte = np.where(mant > 0.5, ex, ex - 1) + 127
    byte = np.clip(np.where(amax > 0, byte, 1), 1, 254)
    scaled = (w * np.exp2(127.0 - byte)[:, None, :]).reshape(k, n).astype(np.float32)
    by_word = np.ascontiguousarray(scaled.reshape(k // 512, 128, 4, n).transpose(0, 1, 3, 2))
    if fmt == "e4m3":
        words = by_word.astype(ml_dtypes.float8_e4m3fn).view(np.uint8)
    else:
        c = by_word.astype(ml_dtypes.float4_e2m1fn).view(np.uint8) & 0xF
        words = c[..., 0::2] | (c[..., 1::2] << 4)
    return np.ascontiguousarray(words), np.ascontiguousarray(byte.astype(np.uint8).reshape(k // 512, 16, n))


def unpack_weight(words, scales, fmt):
    g, p, n, _ = words.shape
    if fmt == "e4m3":
        vals = np.ascontiguousarray(words).view(ml_dtypes.float8_e4m3fn).astype(np.float64)
    else:
        nib = np.empty((g, p, n, 4), np.uint8)
        nib[..., 0::2] = words & 0xF
        nib[..., 1::2] = words >> 4
        vals = E2M1[nib]
    vals = vals * np.repeat(np.exp2(scales.astype(np.float64) - 127.0), 8, axis=1)[..., None]
    return vals.transpose(0, 1, 3, 2).reshape(g * 512, n)


T, D, F1, F2 = 512, 1024, 4096, 1024
EPS = 1e-3
FMT = "e4m3"


def _layernorm(x, gamma, beta):
    mu = np.mean(x, axis=-1, keepdims=True)
    var = np.mean(np.square(x - mu), axis=-1, keepdims=True)
    rsigma = 1.0 / np.sqrt(var + EPS)
    return (x - mu) * rsigma * gamma + beta


def _gelu_tanh(x):
    c = 0.7978845608028654
    return 0.5 * x * (1.0 + np.tanh(c * (x + 0.044715 * x * x * x)))


def setup_inputs():
    s = mx_kscale(D)
    t = mx_kscale(F1)
    u = np.minimum(t, 1.0 / t) ** 2
    inputs = bf(np.random.standard_normal((T, D)) + 0.5)
    gamma = bf((1.0 + 0.1 * np.random.standard_normal(D)) * s)
    beta = bf(0.1 * np.random.standard_normal(D) * s)
    fc1_words, fc1_scales = pack_weight(np.random.standard_normal((D, F1)) / np.sqrt(D) / s[:, None] * u[None, :], FMT)
    fc1_bias = bf(0.1 * np.random.standard_normal(F1) * u)
    fc2_words, fc2_scales = pack_weight(np.random.standard_normal((F1, F2)) * 1.5 / np.sqrt(F1) / u[:, None], FMT)
    fc2_bias = bf(0.1 * np.random.standard_normal(F2))
    return {"inputs": inputs,
            "gamma": gamma,
            "beta": beta,
            "fc1_kernel_words": fc1_words,
            "fc1_kernel_scales": fc1_scales,
            "fc1_bias": fc1_bias,
            "fc2_kernel_words": fc2_words,
            "fc2_kernel_scales": fc2_scales,
            "fc2_bias": fc2_bias}


def reference(inputs, gamma, beta, fc1_kernel_words, fc1_kernel_scales, fc1_bias, fc2_kernel_words, fc2_kernel_scales, fc2_bias):
    ln_out = _layernorm(f64(inputs), f64(gamma), f64(beta))
    fc1_out = (mxq(ln_out, 1, "e4m3") @ unpack_weight(fc1_kernel_words, fc1_kernel_scales, FMT)) + f64(fc1_bias)
    gelu_out = _gelu_tanh(fc1_out)
    fc2_out = (mxq(gelu_out, 1, "e4m3") @ unpack_weight(fc2_kernel_words, fc2_kernel_scales, FMT)) + f64(fc2_bias)
    return fc2_out

@@ -1,0 +1,252 @@
+from contextlib import ExitStack
+
+import concourse.mybir as mybir
+from concourse.masks import make_identity
+
+F32 = mybir.dt.float32
+BF16 = mybir.dt.bfloat16
+I32 = mybir.dt.int32
+U32 = mybir.dt.uint32
+U8 = mybir.dt.uint8
+FP8X4 = mybir.dt.float8_e4m3fn_x4
+ALU = mybir.AluOpType
+ACT = mybir.ActivationFunctionType
+
+P = 128
+PACK = 4
+K_PASS = P * PACK
+N_TILE = 512
+
+T, D, F1, F2 = 512, 1024, 4096, 1024
+EPS = 1e-3
+TOK_TILES = T // P
+D_PASSES = D // K_PASS
+F1_PASSES = F1 // K_PASS
+F2_TILES = F2 // N_TILE
+W1_CHUNK = 1024
+
+FLOPS = 2 * T * D * F1 + 2 * T * F1 * F2
+
+
+def tile_layernormmlp_kernel(
+    tc,
+    inputs,
+    gamma,
+    beta,
+    fc1_kernel_words,
+    fc1_kernel_scales,
+    fc1_bias,
+    fc2_kernel_words,
+    fc2_kernel_scales,
+    fc2_bias,
+    out,
+):
+    nc = tc.nc
+    with ExitStack() as ctx:
+        keep = ctx.enter_context(tc.tile_pool(name="keep", bufs=1))
+        work = ctx.enter_context(tc.tile_pool(name="work", bufs=1))
+        psum = ctx.enter_context(tc.psum_pool(name="psum", bufs=8))
+
+        w1_planes = keep.tile([P, F1], U8, align_bytes=64)
+        w2_planes = keep.tile([P, F1_PASSES // 4, F2], U8, align_bytes=64)
+        nc.vector.memset(w1_planes[:].bitcast(I32), 0)
+        nc.vector.memset(w2_planes[:].rearrange("p a n -> p (a n)").bitcast(I32), 0)
+        eps = keep.tile([P, 1], F32)
+        nc.vector.memset(eps[:], EPS)
+        ident = keep.tile([P, P], F32)
+        make_identity(nc, ident[:])
+
+        x_sb = keep.tile([P, TOK_TILES, D], BF16)
+        for i in range(TOK_TILES):
+            nc.sync.dma_start(out=x_sb[:, i, :], in_=inputs[i * P : (i + 1) * P, :])
+
+        gamma_bf = keep.tile([P, D_PASSES, PACK], BF16)
+        beta_bf = keep.tile([P, D_PASSES, PACK], BF16)
+        nc.scalar.dma_start(out=gamma_bf[:], in_=gamma.rearrange("(c p t) -> p c t", p=P, t=PACK))
+        nc.scalar.dma_start(out=beta_bf[:], in_=beta.rearrange("(c p t) -> p c t", p=P, t=PACK))
+
+        for quad in range(4):
+            nc.sync.dma_start(
+                out=w1_planes[32 * quad : 32 * quad + 4 * D_PASSES, :].bitcast(I32),
+                in_=fc1_kernel_scales[:, 4 * quad : 4 * quad + 4, :].bitcast(I32),
+            )
+
+        w1_words = keep.tile([P, D_PASSES, F1], U32, align_bytes=64)
+        b1_bc = keep.tile([P, F1], BF16)
+        for chunk in range(F1 // W1_CHUNK):
+            cols = slice(chunk * W1_CHUNK, (chunk + 1) * W1_CHUNK)
+            byte_cols = slice(chunk * W1_CHUNK * PACK, (chunk + 1) * W1_CHUNK * PACK)
+            for c in range(D_PASSES):
+                nc.sync.dma_start(
+                    out=w1_words[:, c, cols].bitcast(I32),
+                    in_=fc1_kernel_words[c].rearrange("p n t -> p (n t)")[:, byte_cols].bitcast(I32),
+                )
+            if chunk == 0:
+                nc.sync.dma_start(out=b1_bc[:], in_=fc1_bias.partition_broadcast(P))
+
+        for half in range(F1_PASSES // 4):
+            for quad in range(4):
+                nc.sync.dma_start(
+                    out=w2_planes[32 * quad : 32 * quad + 16, half, :].bitcast(I32),
+                    in_=fc2_kernel_scales[4 * half : 4 * half + 4, 4 * quad : 4 * quad + 4, :].bitcast(I32),
+                )
+        w2_words = keep.tile([P, F1_PASSES, F2], U32, align_bytes=64)
+        for g in range(F1_PASSES):
+            nc.sync.dma_start(
+                out=w2_words[:, g, :].bitcast(I32),
+                in_=fc2_kernel_words[g].rearrange("p n t -> p (n t)").bitcast(I32),
+            )
+        b2_bc = keep.tile([P, F2], BF16)
+        nc.sync.dma_start(out=b2_bc[:], in_=fc2_bias.partition_broadcast(P))
+
+        gamma_f = keep.tile([P, D_PASSES, PACK], F32)
+        beta_f = keep.tile([P, D_PASSES, PACK], F32)
+        nc.vector.tensor_copy(out=gamma_f[:], in_=gamma_bf[:])
+        nc.vector.tensor_copy(out=beta_f[:], in_=beta_bf[:])
+
+        stats = keep.tile([P, TOK_TILES, 2, 6], F32)
+        mean_var = keep.tile([P, TOK_TILES, 2], F32)
+        std = keep.tile([P, TOK_TILES], F32)
+        rstd = keep.tile([P, TOK_TILES], F32)
+        shift = keep.tile([P, TOK_TILES], F32)
+        xhat = keep.tile([P, TOK_TILES, D_PASSES, PACK, P], F32)
+        ln_banks = [
+            psum.tile([P, T], F32, tag="bank", name="ln_bank%d" % k) for k in range(D_PASSES * PACK)
+        ]
+        for i in range(TOK_TILES):
+            for half in range(2):
+                nc.vector.bn_stats(
+                    out=stats[:, i, half, :], in_=x_sb[:, i, half * 512 : (half + 1) * 512]
+                )
+            nc.vector.bn_aggr(
+                out=mean_var[:, i, :], in_=stats[:, i, :, :].rearrange("p h s -> p (h s)")
+            )
+            nc.scalar.activation(
+                out=std[:, i : i + 1], in_=mean_var[:, i, 1:2], func=ACT.Sqrt, bias=eps[:, 0:1], scale=1.0
+            )
+            nc.vector.reciprocal(out=rstd[:, i : i + 1], in_=std[:, i : i + 1])
+            nc.vector.scalar_tensor_tensor(
+                out=shift[:, i : i + 1],
+                in0=mean_var[:, i, 0:1],
+                scalar=-1.0,
+                in1=rstd[:, i : i + 1],
+                op0=ALU.mult,
+                op1=ALU.mult,
+            )
+            nc.scalar.activation(
+                out=xhat[:, i, :, :, :],
+                in_=x_sb[:, i, :].rearrange("p (c q t) -> p c t q", c=D_PASSES, t=PACK),
+                func=ACT.Identity,
+                bias=shift[:, i : i + 1],
+                scale=rstd[:, i : i + 1],
+            )
+            for c in range(D_PASSES):
+                for t in range(PACK):
+                    nc.tensor.transpose(
+                        ln_banks[c * PACK + t][:, i * P : (i + 1) * P], xhat[:, i, c, t, :], ident[:]
+                    )
+
+        ln_planes = keep.tile([P, D_PASSES, PACK, T], BF16)
+        ln_grouped = keep.tile([P, D_PASSES, T, PACK], BF16, align_bytes=64)
+        ln_words = keep.tile([P, D_PASSES, T], U32, align_bytes=64)
+        ln_scales = keep.tile([P, D_PASSES, T], U8, align_bytes=64)
+        for c in range(D_PASSES):
+            for t in range(PACK):
+                if t % 2 == 0:
+                    nc.scalar.activation(
+                        out=ln_planes[:, c, t, :],
+                        in_=ln_banks[c * PACK + t][:],
+                        func=ACT.Identity,
+                        bias=beta_f[:, c, t : t + 1],
+                        scale=gamma_f[:, c, t : t + 1],
+                    )
+                else:
+                    nc.vector.tensor_scalar(
+                        out=ln_planes[:, c, t, :],
+                        in0=ln_banks[c * PACK + t][:],
+                        scalar1=gamma_f[:, c, t : t + 1],
+                        scalar2=beta_f[:, c, t : t + 1],
+                        op0=ALU.mult,
+                        op1=ALU.add,
+                    )
+            nc.vector.tensor_copy(
+                out=ln_grouped[:, c, :, :], in_=ln_planes[:, c, :, :].rearrange("p t w -> p w t")
+            )
+        for c in range(D_PASSES):
+            nc.vector.quantize_mx(
+                out=ln_words[:, c, :].bitcast(FP8X4),
+                scales=ln_scales[:, c, :],
+                in_=ln_grouped[:, c, :, :].rearrange("p w t -> p (w t)"),
+            )
+
+        h_words = keep.tile([P, F1_PASSES, T], U32, align_bytes=64)
+        h_scales = keep.tile([P, F1_PASSES, T], U8, align_bytes=64)
+
+        def fc1_group(g):
+            cols = slice(g * K_PASS, (g + 1) * K_PASS)
+            pre_tiles = []
+            for i in range(TOK_TILES):
+                toks = slice(i * P, (i + 1) * P)
+                acc = psum.tile([P, N_TILE], F32, tag="bank", name="fc1_acc")
+                for c in range(D_PASSES):
+                    nc.tensor.matmul_mx(
+                        out=acc[:],
+                        lhsT=ln_words[:, c, toks].bitcast(FP8X4),
+                        lhsT_scale=ln_scales[:, c, toks],
+                        rhs=w1_words[:, c, cols].bitcast(FP8X4),
+                        rhs_scale=w1_planes[4 * c : P, cols],
+                        start=(c == 0),
+                        stop=(c == D_PASSES - 1),
+                    )
+                pre = work.tile([P, PACK, P], F32, tag="pre", bufs=12, name="pre")
+                nc.vector.tensor_tensor(
+                    out=pre[:],
+                    in0=acc[:].rearrange("p (q t) -> p t q", t=PACK),
+                    in1=b1_bc[:, cols].rearrange("p (q t) -> p t q", t=PACK),
+                    op=ALU.add,
+                )
+                pre_tiles.append(pre)
+            return pre_tiles
+
+        def gelu_group(g, pre_tiles):
+            h_grouped = work.tile([P, TOK_TILES, P, PACK], BF16, tag="h_grouped", bufs=3, align_bytes=64, name="h_grouped")
+            for i in range(TOK_TILES):
+                turned = psum.tile([P, PACK, P], F32, tag="bank", name="turned")
+                for t in range(PACK):
+                    nc.tensor.transpose(turned[:, t, :], pre_tiles[i][:, t, :], ident[:])
+                nc.scalar.activation(
+                    out=h_grouped[:, i, :, :],
+                    in_=turned[:].rearrange("p t w -> p w t"),
+                    func=ACT.Gelu_apprx_tanh,
+                )
+            nc.vector.quantize_mx(
+                out=h_words[:, g, :].bitcast(FP8X4),
+                scales=h_scales[:, g, :],
+                in_=h_grouped[:].rearrange("p i w t -> p (i w t)"),
+            )
+
+        pre_next = fc1_group(0)
+        for g in range(F1_PASSES):
+            pre_now = pre_next
+            if g + 1 < F1_PASSES:
+                pre_next = fc1_group(g + 1)
+            gelu_group(g, pre_now)
+
+        for i in range(TOK_TILES):
+            toks = slice(i * P, (i + 1) * P)
+            for j in range(F2_TILES):
+                cols = slice(j * N_TILE, (j + 1) * N_TILE)
+                acc2 = psum.tile([P, N_TILE], F32, tag="bank", name="fc2_acc")
+                for g in range(F1_PASSES):
+                    nc.tensor.matmul_mx(
+                        out=acc2[:],
+                        lhsT=h_words[:, g, toks].bitcast(FP8X4),
+                        lhsT_scale=h_scales[:, g, toks],
+                        rhs=w2_words[:, g, cols].bitcast(FP8X4),
+                        rhs_scale=w2_planes[4 * (g % 4) : P, g // 4, cols],
+                        start=(g == 0),
+                        stop=(g == F1_PASSES - 1),
+                    )
+                res = work.tile([P, N_TILE], F32, tag="res", bufs=4, name="res")
+                nc.vector.tensor_tensor(out=res[:], in0=acc2[:], in1=b2_bc[:, cols], op=ALU.add)
+                nc.sync.dma_start(out=out[toks, cols], in_=res[:])

@@ -46,6 +46,7 @@ def tile_layernormmlp_kernel(
         keep = ctx.enter_context(tc.tile_pool(name="keep", bufs=1))
         work = ctx.enter_context(tc.tile_pool(name="work", bufs=1))
         psum = ctx.enter_context(tc.psum_pool(name="psum", bufs=8))
+        ctx.enter_context(tc.manual_schedule())
 
         w1_planes = keep.tile([P, F1], U8, align_bytes=64)
         w2_planes = keep.tile([P, F1_PASSES // 4, F2], U8, align_bytes=64)
@@ -99,11 +100,6 @@ def tile_layernormmlp_kernel(
         b2_bc = keep.tile([P, F2], BF16)
         nc.sync.dma_start(out=b2_bc[:], in_=fc2_bias.partition_broadcast(P))
 
-        gamma_f = keep.tile([P, D_PASSES, PACK], F32)
-        beta_f = keep.tile([P, D_PASSES, PACK], F32)
-        nc.vector.tensor_copy(out=gamma_f[:], in_=gamma_bf[:])
-        nc.vector.tensor_copy(out=beta_f[:], in_=beta_bf[:])
-
         stats = keep.tile([P, TOK_TILES, 2, 6], F32)
         mean_var = keep.tile([P, TOK_TILES, 2], F32)
         std = keep.tile([P, TOK_TILES], F32)
@@ -113,7 +109,8 @@ def tile_layernormmlp_kernel(
         ln_banks = [
             psum.tile([P, T], F32, tag="bank", name="ln_bank%d" % k) for k in range(D_PASSES * PACK)
         ]
-        for i in range(TOK_TILES):
+
+        def statistics(i):
             for half in range(2):
                 nc.vector.bn_stats(
                     out=stats[:, i, half, :], in_=x_sb[:, i, half * 512 : (half + 1) * 512]
@@ -124,6 +121,8 @@ def tile_layernormmlp_kernel(
             nc.scalar.activation(
                 out=std[:, i : i + 1], in_=mean_var[:, i, 1:2], func=ACT.Sqrt, bias=eps[:, 0:1], scale=1.0
             )
+
+        def normalise_and_turn(i):
             nc.vector.reciprocal(out=rstd[:, i : i + 1], in_=std[:, i : i + 1])
             nc.vector.scalar_tensor_tensor(
                 out=shift[:, i : i + 1],
@@ -145,6 +144,17 @@ def tile_layernormmlp_kernel(
                     nc.tensor.transpose(
                         ln_banks[c * PACK + t][:, i * P : (i + 1) * P], xhat[:, i, c, t, :], ident[:]
                     )
+
+        for i in range(TOK_TILES + 1):
+            if i < TOK_TILES:
+                statistics(i)
+            if i > 0:
+                normalise_and_turn(i - 1)
+
+        gamma_f = keep.tile([P, D_PASSES, PACK], F32)
+        beta_f = keep.tile([P, D_PASSES, PACK], F32)
+        nc.vector.tensor_copy(out=gamma_f[:], in_=gamma_bf[:])
+        nc.vector.tensor_copy(out=beta_f[:], in_=beta_bf[:])
 
         ln_planes = keep.tile([P, D_PASSES, PACK, T], BF16)
         ln_grouped = keep.tile([P, D_PASSES, T, PACK], BF16, align_bytes=64)
@@ -170,7 +180,8 @@ def tile_layernormmlp_kernel(
                         op1=ALU.add,
                     )
             nc.vector.tensor_copy(
-                out=ln_grouped[:, c, :, :], in_=ln_planes[:, c, :, :].rearrange("p t w -> p w t")
+                out=ln_grouped[:, c, :, :].rearrange("p (a b) t -> p a t b", b=4),
+                in_=ln_planes[:, c, :, :].rearrange("p t (a b) -> p a t b", b=4),
             )
         for c in range(D_PASSES):
             nc.vector.quantize_mx(
@@ -219,18 +230,24 @@ def tile_layernormmlp_kernel(
                     in_=turned[:].rearrange("p t w -> p w t"),
                     func=ACT.Gelu_apprx_tanh,
                 )
+            return h_grouped
+
+        def quantise_group(g, h_grouped):
             nc.vector.quantize_mx(
                 out=h_words[:, g, :].bitcast(FP8X4),
                 scales=h_scales[:, g, :],
                 in_=h_grouped[:].rearrange("p i w t -> p (i w t)"),
             )
 
-        pre_next = fc1_group(0)
+        pre_tiles = {0: fc1_group(0)}
+        h_tiles = {}
         for g in range(F1_PASSES):
-            pre_now = pre_next
             if g + 1 < F1_PASSES:
-                pre_next = fc1_group(g + 1)
-            gelu_group(g, pre_now)
+                pre_tiles[g + 1] = fc1_group(g + 1)
+            h_tiles[g] = gelu_group(g, pre_tiles[g])
+            if g > 0:
+                quantise_group(g - 1, h_tiles[g - 1])
+        quantise_group(F1_PASSES - 1, h_tiles[F1_PASSES - 1])
 
         for i in range(TOK_TILES):
             toks = slice(i * P, (i + 1) * P)

@@ -133,8 +133,8 @@ def tile_layernormmlp_kernel(
                 op1=ALU.mult,
             )
             nc.scalar.activation(
-                out=xhat[:, i, :, :, :],
-                in_=x_sb[:, i, :].rearrange("p (c q t) -> p c t q", c=D_PASSES, t=PACK),
+                out=xhat[:, i, :, :, :].rearrange("p c t q -> p c q t"),
+                in_=x_sb[:, i, :].rearrange("p (c q t) -> p c q t", c=D_PASSES, t=PACK),
                 func=ACT.Identity,
                 bias=shift[:, i : i + 1],
                 scale=rstd[:, i : i + 1],
@@ -211,9 +211,9 @@ def tile_layernormmlp_kernel(
                     )
                 pre = work.tile([P, PACK, P], F32, tag="pre", bufs=12, name="pre")
                 nc.vector.tensor_tensor(
-                    out=pre[:],
-                    in0=acc[:].rearrange("p (q t) -> p t q", t=PACK),
-                    in1=b1_bc[:, cols].rearrange("p (q t) -> p t q", t=PACK),
+                    out=pre[:].rearrange("p t q -> p q t"),
+                    in0=acc[:].rearrange("p (q t) -> p q t", t=PACK),
+                    in1=b1_bc[:, cols].rearrange("p (q t) -> p q t", t=PACK),
                     op=ALU.add,
                 )
                 pre_tiles.append(pre)

@@ -16,14 +16,18 @@ P = 128
 PACK = 4
 K_PASS = P * PACK
 N_TILE = 512
+BANKS = 8
 
 T, D, F1, F2 = 512, 1024, 4096, 1024
 EPS = 1e-3
-TOK_TILES = T // P
 D_PASSES = D // K_PASS
 F1_PASSES = F1 // K_PASS
 F2_TILES = F2 // N_TILE
-W1_CHUNK = 1024
+HALVES = 2
+HALF_TILES = T // P // HALVES
+HALF = HALF_TILES * P
+PAIR = 2
+PAIRS = F1_PASSES // PAIR
 
 FLOPS = 2 * T * D * F1 + 2 * T * F1 * F2
 
@@ -45,7 +49,7 @@ def tile_layernormmlp_kernel(
     with ExitStack() as ctx:
         keep = ctx.enter_context(tc.tile_pool(name="keep", bufs=1))
         work = ctx.enter_context(tc.tile_pool(name="work", bufs=1))
-        psum = ctx.enter_context(tc.psum_pool(name="psum", bufs=8))
+        psum = ctx.enter_context(tc.psum_pool(name="psum", bufs=BANKS))
         ctx.enter_context(tc.manual_schedule())
 
         w1_planes = keep.tile([P, F1], U8, align_bytes=64)
@@ -57,9 +61,11 @@ def tile_layernormmlp_kernel(
         ident = keep.tile([P, P], F32)
         make_identity(nc, ident[:])
 
-        x_sb = keep.tile([P, TOK_TILES, D], BF16)
-        for i in range(TOK_TILES):
-            nc.sync.dma_start(out=x_sb[:, i, :], in_=inputs[i * P : (i + 1) * P, :])
+        x_sb = keep.tile([P, HALVES, HALF_TILES, D], BF16)
+        for half in range(HALVES):
+            for il in range(HALF_TILES):
+                row = (half * HALF_TILES + il) * P
+                nc.sync.dma_start(out=x_sb[:, half, il, :], in_=inputs[row : row + P, :])
 
         gamma_bf = keep.tile([P, D_PASSES, PACK], BF16)
         beta_bf = keep.tile([P, D_PASSES, PACK], BF16)
@@ -74,22 +80,22 @@ def tile_layernormmlp_kernel(
 
         w1_words = keep.tile([P, D_PASSES, F1], U32, align_bytes=64)
         b1_bc = keep.tile([P, F1], BF16)
-        for chunk in range(F1 // W1_CHUNK):
-            cols = slice(chunk * W1_CHUNK, (chunk + 1) * W1_CHUNK)
-            byte_cols = slice(chunk * W1_CHUNK * PACK, (chunk + 1) * W1_CHUNK * PACK)
+        for pair in range(PAIRS):
+            cols = slice(pair * PAIR * K_PASS, (pair + 1) * PAIR * K_PASS)
+            byte_cols = slice(pair * PAIR * K_PASS * PACK, (pair + 1) * PAIR * K_PASS * PACK)
             for c in range(D_PASSES):
                 nc.sync.dma_start(
                     out=w1_words[:, c, cols].bitcast(I32),
                     in_=fc1_kernel_words[c].rearrange("p n t -> p (n t)")[:, byte_cols].bitcast(I32),
                 )
-            if chunk == 0:
+            if pair == 0:
                 nc.sync.dma_start(out=b1_bc[:], in_=fc1_bias.partition_broadcast(P))
 
-        for half in range(F1_PASSES // 4):
+        for four in range(F1_PASSES // 4):
             for quad in range(4):
                 nc.sync.dma_start(
-                    out=w2_planes[32 * quad : 32 * quad + 16, half, :].bitcast(I32),
-                    in_=fc2_kernel_scales[4 * half : 4 * half + 4, 4 * quad : 4 * quad + 4, :].bitcast(I32),
+                    out=w2_planes[32 * quad : 32 * quad + 16, four, :].bitcast(I32),
+                    in_=fc2_kernel_scales[4 * four : 4 * four + 4, 4 * quad : 4 * quad + 4, :].bitcast(I32),
                 )
         w2_words = keep.tile([P, F1_PASSES, F2], U32, align_bytes=64)
         for g in range(F1_PASSES):
@@ -100,170 +106,199 @@ def tile_layernormmlp_kernel(
         b2_bc = keep.tile([P, F2], BF16)
         nc.sync.dma_start(out=b2_bc[:], in_=fc2_bias.partition_broadcast(P))
 
-        stats = keep.tile([P, TOK_TILES, 2, 6], F32)
-        mean_var = keep.tile([P, TOK_TILES, 2], F32)
-        std = keep.tile([P, TOK_TILES], F32)
-        rstd = keep.tile([P, TOK_TILES], F32)
-        shift = keep.tile([P, TOK_TILES], F32)
-        xhat = keep.tile([P, TOK_TILES, D_PASSES, PACK, P], F32)
-        ln_banks = [
-            psum.tile([P, T], F32, tag="bank", name="ln_bank%d" % k) for k in range(D_PASSES * PACK)
-        ]
-
-        def statistics(i):
-            for half in range(2):
-                nc.vector.bn_stats(
-                    out=stats[:, i, half, :], in_=x_sb[:, i, half * 512 : (half + 1) * 512]
-                )
-            nc.vector.bn_aggr(
-                out=mean_var[:, i, :], in_=stats[:, i, :, :].rearrange("p h s -> p (h s)")
-            )
-            nc.scalar.activation(
-                out=std[:, i : i + 1], in_=mean_var[:, i, 1:2], func=ACT.Sqrt, bias=eps[:, 0:1], scale=1.0
-            )
-
-        def normalise_and_turn(i):
-            nc.vector.reciprocal(out=rstd[:, i : i + 1], in_=std[:, i : i + 1])
-            nc.vector.scalar_tensor_tensor(
-                out=shift[:, i : i + 1],
-                in0=mean_var[:, i, 0:1],
-                scalar=-1.0,
-                in1=rstd[:, i : i + 1],
-                op0=ALU.mult,
-                op1=ALU.mult,
-            )
-            nc.scalar.activation(
-                out=xhat[:, i, :, :, :].rearrange("p c t q -> p c q t"),
-                in_=x_sb[:, i, :].rearrange("p (c q t) -> p c q t", c=D_PASSES, t=PACK),
-                func=ACT.Identity,
-                bias=shift[:, i : i + 1],
-                scale=rstd[:, i : i + 1],
-            )
-            for c in range(D_PASSES):
-                for t in range(PACK):
-                    nc.tensor.transpose(
-                        ln_banks[c * PACK + t][:, i * P : (i + 1) * P], xhat[:, i, c, t, :], ident[:]
-                    )
-
-        for i in range(TOK_TILES + 1):
-            if i < TOK_TILES:
-                statistics(i)
-            if i > 0:
-                normalise_and_turn(i - 1)
-
         gamma_f = keep.tile([P, D_PASSES, PACK], F32)
         beta_f = keep.tile([P, D_PASSES, PACK], F32)
         nc.vector.tensor_copy(out=gamma_f[:], in_=gamma_bf[:])
         nc.vector.tensor_copy(out=beta_f[:], in_=beta_bf[:])
 
-        ln_planes = keep.tile([P, D_PASSES, PACK, T], BF16)
-        ln_grouped = keep.tile([P, D_PASSES, T, PACK], BF16, align_bytes=64)
-        ln_words = keep.tile([P, D_PASSES, T], U32, align_bytes=64)
-        ln_scales = keep.tile([P, D_PASSES, T], U8, align_bytes=64)
-        for c in range(D_PASSES):
-            for t in range(PACK):
-                if t % 2 == 0:
-                    nc.scalar.activation(
-                        out=ln_planes[:, c, t, :],
-                        in_=ln_banks[c * PACK + t][:],
-                        func=ACT.Identity,
-                        bias=beta_f[:, c, t : t + 1],
-                        scale=gamma_f[:, c, t : t + 1],
-                    )
-                else:
-                    nc.vector.tensor_scalar(
-                        out=ln_planes[:, c, t, :],
-                        in0=ln_banks[c * PACK + t][:],
-                        scalar1=gamma_f[:, c, t : t + 1],
-                        scalar2=beta_f[:, c, t : t + 1],
-                        op0=ALU.mult,
-                        op1=ALU.add,
-                    )
-            nc.vector.tensor_copy(
-                out=ln_grouped[:, c, :, :].rearrange("p (a b) t -> p a t b", b=4),
-                in_=ln_planes[:, c, :, :].rearrange("p t (a b) -> p a t b", b=4),
-            )
-        for c in range(D_PASSES):
-            nc.vector.quantize_mx(
-                out=ln_words[:, c, :].bitcast(FP8X4),
-                scales=ln_scales[:, c, :],
-                in_=ln_grouped[:, c, :, :].rearrange("p w t -> p (w t)"),
-            )
+        stats = keep.tile([P, HALVES, HALF_TILES, 2, 6], F32)
+        mean_var = keep.tile([P, HALVES, HALF_TILES, 2], F32)
+        std = keep.tile([P, HALVES, HALF_TILES], F32)
+        rstd = keep.tile([P, HALVES, HALF_TILES], F32)
+        shift = keep.tile([P, HALVES, HALF_TILES], F32)
+        xhat = keep.tile([P, HALVES, HALF_TILES, D_PASSES, PACK, P], F32)
+        ln_planes = keep.tile([P, HALVES, D_PASSES, PACK, HALF], BF16)
+        ln_grouped = keep.tile([P, HALVES, D_PASSES, HALF, PACK], BF16, align_bytes=64)
+        ln_words = keep.tile([P, HALVES, D_PASSES, HALF], U32, align_bytes=64)
+        ln_scales = keep.tile([P, HALVES, D_PASSES, HALF], U8, align_bytes=64)
 
-        h_words = keep.tile([P, F1_PASSES, T], U32, align_bytes=64)
-        h_scales = keep.tile([P, F1_PASSES, T], U8, align_bytes=64)
-
-        def fc1_group(g):
-            cols = slice(g * K_PASS, (g + 1) * K_PASS)
-            pre_tiles = []
-            for i in range(TOK_TILES):
-                toks = slice(i * P, (i + 1) * P)
-                acc = psum.tile([P, N_TILE], F32, tag="bank", name="fc1_acc")
-                for c in range(D_PASSES):
-                    nc.tensor.matmul_mx(
-                        out=acc[:],
-                        lhsT=ln_words[:, c, toks].bitcast(FP8X4),
-                        lhsT_scale=ln_scales[:, c, toks],
-                        rhs=w1_words[:, c, cols].bitcast(FP8X4),
-                        rhs_scale=w1_planes[4 * c : P, cols],
-                        start=(c == 0),
-                        stop=(c == D_PASSES - 1),
-                    )
-                pre = work.tile([P, PACK, P], F32, tag="pre", bufs=12, name="pre")
-                nc.vector.tensor_tensor(
-                    out=pre[:].rearrange("p t q -> p q t"),
-                    in0=acc[:].rearrange("p (q t) -> p q t", t=PACK),
-                    in1=b1_bc[:, cols].rearrange("p (q t) -> p q t", t=PACK),
-                    op=ALU.add,
+        def statistics(half, il):
+            for part in range(2):
+                nc.vector.bn_stats(
+                    out=stats[:, half, il, part, :],
+                    in_=x_sb[:, half, il, part * 512 : (part + 1) * 512],
                 )
-                pre_tiles.append(pre)
+            nc.vector.bn_aggr(
+                out=mean_var[:, half, il, :],
+                in_=stats[:, half, il, :, :].rearrange("p h s -> p (h s)"),
+            )
+
+        def normalise(half, il):
+            one = slice(il, il + 1)
+            nc.scalar.activation(
+                out=std[:, half, one], in_=mean_var[:, half, il, 1:2], func=ACT.Sqrt, bias=eps[:, 0:1], scale=1.0
+            )
+            nc.vector.reciprocal(out=rstd[:, half, one], in_=std[:, half, one])
+            nc.vector.scalar_tensor_tensor(
+                out=shift[:, half, one],
+                in0=mean_var[:, half, il, 0:1],
+                scalar=-1.0,
+                in1=rstd[:, half, one],
+                op0=ALU.mult,
+                op1=ALU.mult,
+            )
+            nc.scalar.activation(
+                out=xhat[:, half, il, :, :, :].rearrange("p c t q -> p c q t"),
+                in_=x_sb[:, half, il, :].rearrange("p (c q t) -> p c q t", c=D_PASSES, t=PACK),
+                func=ACT.Identity,
+                bias=shift[:, half, one],
+                scale=rstd[:, half, one],
+            )
+
+        def turn_ln(half):
+            banks = [
+                psum.tile([P, 2, HALF], F32, tag="bank", name="ln_bank%d" % k)
+                for k in range(D_PASSES * PACK // 2)
+            ]
+            for il in range(HALF_TILES):
+                for c in range(D_PASSES):
+                    for t in range(PACK):
+                        plane = c * PACK + t
+                        nc.tensor.transpose(
+                            banks[plane // 2][:, plane % 2, il * P : (il + 1) * P],
+                            xhat[:, half, il, c, t, :],
+                            ident[:],
+                        )
+            for c in range(D_PASSES):
+                for t in range(PACK):
+                    plane = c * PACK + t
+                    if t < PACK - 1:
+                        nc.scalar.activation(
+                            out=ln_planes[:, half, c, t, :],
+                            in_=banks[plane // 2][:, plane % 2, :],
+                            func=ACT.Identity,
+                            bias=beta_f[:, c, t : t + 1],
+                            scale=gamma_f[:, c, t : t + 1],
+                        )
+                    else:
+                        nc.vector.tensor_scalar(
+                            out=ln_planes[:, half, c, t, :],
+                            in0=banks[plane // 2][:, plane % 2, :],
+                            scalar1=gamma_f[:, c, t : t + 1],
+                            scalar2=beta_f[:, c, t : t + 1],
+                            op0=ALU.mult,
+                            op1=ALU.add,
+                        )
+
+        def quantise_ln(half):
+            for c in range(D_PASSES):
+                nc.vector.tensor_copy(
+                    out=ln_grouped[:, half, c, :, :].rearrange("p (a b) t -> p a t b", b=4),
+                    in_=ln_planes[:, half, c, :, :].rearrange("p t (a b) -> p a t b", b=4),
+                )
+            nc.vector.quantize_mx(
+                out=ln_words[:, half, :, :].rearrange("p c w -> p (c w)").bitcast(FP8X4),
+                scales=ln_scales[:, half, :, :].rearrange("p c w -> p (c w)"),
+                in_=ln_grouped[:, half, :, :, :].rearrange("p c w t -> p (c w t)"),
+            )
+
+        h_words = keep.tile([P, HALVES, F1_PASSES, HALF], U32, align_bytes=64)
+        h_scales = keep.tile([P, HALVES, F1_PASSES, HALF], U8, align_bytes=64)
+
+        def fc1_unit(half, pair):
+            pre_tiles = []
+            for gl in range(PAIR):
+                g = pair * PAIR + gl
+                cols = slice(g * K_PASS, (g + 1) * K_PASS)
+                for il in range(HALF_TILES):
+                    toks = slice(il * P, (il + 1) * P)
+                    acc = psum.tile([P, N_TILE], F32, tag="bank", name="fc1_acc")
+                    for c in range(D_PASSES):
+                        nc.tensor.matmul_mx(
+                            out=acc[:],
+                            lhsT=ln_words[:, half, c, toks].bitcast(FP8X4),
+                            lhsT_scale=ln_scales[:, half, c, toks],
+                            rhs=w1_words[:, c, cols].bitcast(FP8X4),
+                            rhs_scale=w1_planes[4 * c : P, cols],
+                            start=(c == 0),
+                            stop=(c == D_PASSES - 1),
+                        )
+                    pre = work.tile([P, PACK, P], F32, tag="pre", bufs=12, name="pre")
+                    nc.vector.tensor_tensor(
+                        out=pre[:].rearrange("p t q -> p q t"),
+                        in0=acc[:].rearrange("p (q t) -> p q t", t=PACK),
+                        in1=b1_bc[:, cols].rearrange("p (q t) -> p q t", t=PACK),
+                        op=ALU.add,
+                    )
+                    pre_tiles.append(pre)
             return pre_tiles
 
-        def gelu_group(g, pre_tiles):
-            h_grouped = work.tile([P, TOK_TILES, P, PACK], BF16, tag="h_grouped", bufs=3, align_bytes=64, name="h_grouped")
-            for i in range(TOK_TILES):
+        def gelu_unit(pre_tiles):
+            h_grouped = work.tile(
+                [P, PAIR * HALF_TILES, P, PACK], BF16, tag="h_grouped", bufs=3, align_bytes=64, name="h_grouped"
+            )
+            for k in range(PAIR * HALF_TILES):
                 turned = psum.tile([P, PACK, P], F32, tag="bank", name="turned")
                 for t in range(PACK):
-                    nc.tensor.transpose(turned[:, t, :], pre_tiles[i][:, t, :], ident[:])
+                    nc.tensor.transpose(turned[:, t, :], pre_tiles[k][:, t, :], ident[:])
                 nc.scalar.activation(
-                    out=h_grouped[:, i, :, :],
+                    out=h_grouped[:, k, :, :],
                     in_=turned[:].rearrange("p t w -> p w t"),
                     func=ACT.Gelu_apprx_tanh,
                 )
             return h_grouped
 
-        def quantise_group(g, h_grouped):
+        def quantise_unit(half, pair, h_grouped):
+            groups = slice(pair * PAIR, (pair + 1) * PAIR)
             nc.vector.quantize_mx(
-                out=h_words[:, g, :].bitcast(FP8X4),
-                scales=h_scales[:, g, :],
-                in_=h_grouped[:].rearrange("p i w t -> p (i w t)"),
+                out=h_words[:, half, groups, :].rearrange("p g w -> p (g w)").bitcast(FP8X4),
+                scales=h_scales[:, half, groups, :].rearrange("p g w -> p (g w)"),
+                in_=h_grouped[:].rearrange("p k w t -> p (k w t)"),
             )
 
-        pre_tiles = {0: fc1_group(0)}
-        h_tiles = {}
-        for g in range(F1_PASSES):
-            if g + 1 < F1_PASSES:
-                pre_tiles[g + 1] = fc1_group(g + 1)
-            h_tiles[g] = gelu_group(g, pre_tiles[g])
-            if g > 0:
-                quantise_group(g - 1, h_tiles[g - 1])
-        quantise_group(F1_PASSES - 1, h_tiles[F1_PASSES - 1])
+        for il in range(HALF_TILES):
+            statistics(0, il)
+            normalise(0, il)
+        for il in range(HALF_TILES):
+            statistics(1, il)
+        turn_ln(0)
+        quantise_ln(0)
+        for il in range(HALF_TILES):
+            normalise(1, il)
 
-        for i in range(TOK_TILES):
-            toks = slice(i * P, (i + 1) * P)
-            for j in range(F2_TILES):
-                cols = slice(j * N_TILE, (j + 1) * N_TILE)
-                acc2 = psum.tile([P, N_TILE], F32, tag="bank", name="fc2_acc")
-                for g in range(F1_PASSES):
-                    nc.tensor.matmul_mx(
-                        out=acc2[:],
-                        lhsT=h_words[:, g, toks].bitcast(FP8X4),
-                        lhsT_scale=h_scales[:, g, toks],
-                        rhs=w2_words[:, g, cols].bitcast(FP8X4),
-                        rhs_scale=w2_planes[4 * (g % 4) : P, g // 4, cols],
-                        start=(g == 0),
-                        stop=(g == F1_PASSES - 1),
-                    )
-                res = work.tile([P, N_TILE], F32, tag="res", bufs=4, name="res")
-                nc.vector.tensor_tensor(out=res[:], in0=acc2[:], in1=b2_bc[:, cols], op=ALU.add)
-                nc.sync.dma_start(out=out[toks, cols], in_=res[:])
+        units = [(half, pair) for half in range(HALVES) for pair in range(PAIRS)]
+        pre_of = {0: fc1_unit(0, 0)}
+        h_of = {}
+        for u in range(len(units)):
+            if u + 1 < len(units):
+                pre_of[u + 1] = fc1_unit(units[u + 1][0], units[u + 1][1])
+            h_of[u] = gelu_unit(pre_of[u])
+            if u == 0:
+                turn_ln(1)
+            if u == 1:
+                quantise_ln(1)
+            if u > 0:
+                quantise_unit(units[u - 1][0], units[u - 1][1], h_of[u - 1])
+        last = len(units) - 1
+        quantise_unit(units[last][0], units[last][1], h_of[last])
+
+        for half in range(HALVES):
+            for il in range(HALF_TILES):
+                toks = slice(il * P, (il + 1) * P)
+                row = (half * HALF_TILES + il) * P
+                for j in range(F2_TILES):
+                    cols = slice(j * N_TILE, (j + 1) * N_TILE)
+                    acc2 = psum.tile([P, N_TILE], F32, tag="bank", name="fc2_acc")
+                    for g in range(F1_PASSES):
+                        nc.tensor.matmul_mx(
+                            out=acc2[:],
+                            lhsT=h_words[:, half, g, toks].bitcast(FP8X4),
+                            lhsT_scale=h_scales[:, half, g, toks],
+                            rhs=w2_words[:, g, cols].bitcast(FP8X4),
+                            rhs_scale=w2_planes[4 * (g % 4) : P, g // 4, cols],
+                            start=(g == 0),
+                            stop=(g == F1_PASSES - 1),
+                        )
+                    res = work.tile([P, N_TILE], F32, tag="res", bufs=4, name="res")
+                    nc.vector.tensor_tensor(out=res[:], in0=acc2[:], in1=b2_bc[:, cols], op=ALU.add)
+                    nc.sync.dma_start(out=out[row : row + P, cols], in_=res[:])

@@ -16,18 +16,17 @@ P = 128
 PACK = 4
 K_PASS = P * PACK
 N_TILE = 512
-BANKS = 8
 
 T, D, F1, F2 = 512, 1024, 4096, 1024
 EPS = 1e-3
+TOK_TILES = T // P
 D_PASSES = D // K_PASS
 F1_PASSES = F1 // K_PASS
+F1_TILES = F1 // P
 F2_TILES = F2 // N_TILE
-HALVES = 2
-HALF_TILES = T // P // HALVES
-HALF = HALF_TILES * P
-PAIR = 2
-PAIRS = F1_PASSES // PAIR
+W1_CHUNK = 1024
+PARKED = 4
+LAG = 4
 
 FLOPS = 2 * T * D * F1 + 2 * T * F1 * F2
 
@@ -49,7 +48,7 @@ def tile_layernormmlp_kernel(
     with ExitStack() as ctx:
         keep = ctx.enter_context(tc.tile_pool(name="keep", bufs=1))
         work = ctx.enter_context(tc.tile_pool(name="work", bufs=1))
-        psum = ctx.enter_context(tc.psum_pool(name="psum", bufs=BANKS))
+        psum = ctx.enter_context(tc.psum_pool(name="psum", bufs=4))
         ctx.enter_context(tc.manual_schedule())
 
         w1_planes = keep.tile([P, F1], U8, align_bytes=64)
@@ -58,38 +57,35 @@ def tile_layernormmlp_kernel(
         nc.vector.memset(w2_planes[:].rearrange("p a n -> p (a n)").bitcast(I32), 0)
         eps = keep.tile([P, 1], F32)
         nc.vector.memset(eps[:], EPS)
+        b1_rows = keep.tile([P, P], BF16)
+        nc.vector.memset(b1_rows[:], 0.0)
         ident = keep.tile([P, P], F32)
         make_identity(nc, ident[:])
 
-        x_sb = keep.tile([P, HALVES, HALF_TILES, D], BF16)
-        for half in range(HALVES):
-            for il in range(HALF_TILES):
-                row = (half * HALF_TILES + il) * P
-                nc.sync.dma_start(out=x_sb[:, half, il, :], in_=inputs[row : row + P, :])
+        x_sb = keep.tile([P, TOK_TILES, D], BF16)
+        for i in range(TOK_TILES):
+            nc.sync.dma_start(out=x_sb[:, i, :], in_=inputs[i * P : (i + 1) * P, :])
 
         gamma_bf = keep.tile([P, D_PASSES, PACK], BF16)
         beta_bf = keep.tile([P, D_PASSES, PACK], BF16)
         nc.scalar.dma_start(out=gamma_bf[:], in_=gamma.rearrange("(c p t) -> p c t", p=P, t=PACK))
         nc.scalar.dma_start(out=beta_bf[:], in_=beta.rearrange("(c p t) -> p c t", p=P, t=PACK))
+        nc.scalar.dma_start(out=b1_rows[0:F1_TILES, :], in_=fc1_bias.rearrange("(j m) -> j m", m=P))
 
         for quad in range(4):
             nc.sync.dma_start(
                 out=w1_planes[32 * quad : 32 * quad + 4 * D_PASSES, :].bitcast(I32),
                 in_=fc1_kernel_scales[:, 4 * quad : 4 * quad + 4, :].bitcast(I32),
             )
-
         w1_words = keep.tile([P, D_PASSES, F1], U32, align_bytes=64)
-        b1_bc = keep.tile([P, F1], BF16)
-        for pair in range(PAIRS):
-            cols = slice(pair * PAIR * K_PASS, (pair + 1) * PAIR * K_PASS)
-            byte_cols = slice(pair * PAIR * K_PASS * PACK, (pair + 1) * PAIR * K_PASS * PACK)
+        for chunk in range(F1 // W1_CHUNK):
+            cols = slice(chunk * W1_CHUNK, (chunk + 1) * W1_CHUNK)
+            byte_cols = slice(chunk * W1_CHUNK * PACK, (chunk + 1) * W1_CHUNK * PACK)
             for c in range(D_PASSES):
                 nc.sync.dma_start(
                     out=w1_words[:, c, cols].bitcast(I32),
                     in_=fc1_kernel_words[c].rearrange("p n t -> p (n t)")[:, byte_cols].bitcast(I32),
                 )
-            if pair == 0:
-                nc.sync.dma_start(out=b1_bc[:], in_=fc1_bias.partition_broadcast(P))
 
         for four in range(F1_PASSES // 4):
             for quad in range(4):
@@ -110,195 +106,189 @@ def tile_layernormmlp_kernel(
         beta_f = keep.tile([P, D_PASSES, PACK], F32)
         nc.vector.tensor_copy(out=gamma_f[:], in_=gamma_bf[:])
         nc.vector.tensor_copy(out=beta_f[:], in_=beta_bf[:])
+        b1_rows_f = keep.tile([P, P], F32)
+        nc.vector.tensor_copy(out=b1_rows_f[:], in_=b1_rows[:])
+        b1_bank = psum.tile([P, P], F32, tag="short", name="b1_bank")
+        nc.tensor.transpose(b1_bank[:], b1_rows_f[:], ident[:])
+        b1_col = keep.tile([P, F1_TILES], F32)
+        nc.vector.tensor_copy(out=b1_col[:], in_=b1_bank[:, 0:F1_TILES])
 
-        stats = keep.tile([P, HALVES, HALF_TILES, 2, 6], F32)
-        mean_var = keep.tile([P, HALVES, HALF_TILES, 2], F32)
-        std = keep.tile([P, HALVES, HALF_TILES], F32)
-        rstd = keep.tile([P, HALVES, HALF_TILES], F32)
-        shift = keep.tile([P, HALVES, HALF_TILES], F32)
-        xhat = keep.tile([P, HALVES, HALF_TILES, D_PASSES, PACK, P], F32)
-        ln_planes = keep.tile([P, HALVES, D_PASSES, PACK, HALF], BF16)
-        ln_grouped = keep.tile([P, HALVES, D_PASSES, HALF, PACK], BF16, align_bytes=64)
-        ln_words = keep.tile([P, HALVES, D_PASSES, HALF], U32, align_bytes=64)
-        ln_scales = keep.tile([P, HALVES, D_PASSES, HALF], U8, align_bytes=64)
+        stats = keep.tile([P, TOK_TILES, 2, 6], F32)
+        mean_var = keep.tile([P, TOK_TILES, 2], F32)
+        std = keep.tile([P, TOK_TILES], F32)
+        rstd = keep.tile([P, TOK_TILES], F32)
+        shift = keep.tile([P, TOK_TILES], F32)
+        xhat = keep.tile([P, TOK_TILES, D_PASSES, PACK, P], F32)
+        ln_banks = [
+            psum.tile([P, T], F32, tag=("short" if k < PACK else "long"), name="ln_bank%d" % k)
+            for k in range(D_PASSES * PACK)
+        ]
 
-        def statistics(half, il):
-            for part in range(2):
+        def statistics(i):
+            for half in range(2):
                 nc.vector.bn_stats(
-                    out=stats[:, half, il, part, :],
-                    in_=x_sb[:, half, il, part * 512 : (part + 1) * 512],
+                    out=stats[:, i, half, :], in_=x_sb[:, i, half * 512 : (half + 1) * 512]
                 )
             nc.vector.bn_aggr(
-                out=mean_var[:, half, il, :],
-                in_=stats[:, half, il, :, :].rearrange("p h s -> p (h s)"),
+                out=mean_var[:, i, :], in_=stats[:, i, :, :].rearrange("p h s -> p (h s)")
+            )
+            nc.scalar.activation(
+                out=std[:, i : i + 1], in_=mean_var[:, i, 1:2], func=ACT.Sqrt, bias=eps[:, 0:1], scale=1.0
             )
 
-        def normalise(half, il):
-            one = slice(il, il + 1)
-            nc.scalar.activation(
-                out=std[:, half, one], in_=mean_var[:, half, il, 1:2], func=ACT.Sqrt, bias=eps[:, 0:1], scale=1.0
-            )
-            nc.vector.reciprocal(out=rstd[:, half, one], in_=std[:, half, one])
+        def normalise_and_turn(i):
+            nc.vector.reciprocal(out=rstd[:, i : i + 1], in_=std[:, i : i + 1])
             nc.vector.scalar_tensor_tensor(
-                out=shift[:, half, one],
-                in0=mean_var[:, half, il, 0:1],
+                out=shift[:, i : i + 1],
+                in0=mean_var[:, i, 0:1],
                 scalar=-1.0,
-                in1=rstd[:, half, one],
+                in1=rstd[:, i : i + 1],
                 op0=ALU.mult,
                 op1=ALU.mult,
             )
             nc.scalar.activation(
-                out=xhat[:, half, il, :, :, :].rearrange("p c t q -> p c q t"),
-                in_=x_sb[:, half, il, :].rearrange("p (c q t) -> p c q t", c=D_PASSES, t=PACK),
+                out=xhat[:, i, :, :, :].rearrange("p c t q -> p c q t"),
+                in_=x_sb[:, i, :].rearrange("p (c q t) -> p c q t", c=D_PASSES, t=PACK),
                 func=ACT.Identity,
-                bias=shift[:, half, one],
-                scale=rstd[:, half, one],
+                bias=shift[:, i : i + 1],
+                scale=rstd[:, i : i + 1],
             )
-
-        def turn_ln(half):
-            banks = [
-                psum.tile([P, 2, HALF], F32, tag="bank", name="ln_bank%d" % k)
-                for k in range(D_PASSES * PACK // 2)
-            ]
-            for il in range(HALF_TILES):
-                for c in range(D_PASSES):
-                    for t in range(PACK):
-                        plane = c * PACK + t
-                        nc.tensor.transpose(
-                            banks[plane // 2][:, plane % 2, il * P : (il + 1) * P],
-                            xhat[:, half, il, c, t, :],
-                            ident[:],
-                        )
             for c in range(D_PASSES):
                 for t in range(PACK):
-                    plane = c * PACK + t
-                    if t < PACK - 1:
-                        nc.scalar.activation(
-                            out=ln_planes[:, half, c, t, :],
-                            in_=banks[plane // 2][:, plane % 2, :],
-                            func=ACT.Identity,
-                            bias=beta_f[:, c, t : t + 1],
-                            scale=gamma_f[:, c, t : t + 1],
-                        )
-                    else:
-                        nc.vector.tensor_scalar(
-                            out=ln_planes[:, half, c, t, :],
-                            in0=banks[plane // 2][:, plane % 2, :],
-                            scalar1=gamma_f[:, c, t : t + 1],
-                            scalar2=beta_f[:, c, t : t + 1],
-                            op0=ALU.mult,
-                            op1=ALU.add,
-                        )
-
-        def quantise_ln(half):
-            for c in range(D_PASSES):
-                nc.vector.tensor_copy(
-                    out=ln_grouped[:, half, c, :, :].rearrange("p (a b) t -> p a t b", b=4),
-                    in_=ln_planes[:, half, c, :, :].rearrange("p t (a b) -> p a t b", b=4),
-                )
-            nc.vector.quantize_mx(
-                out=ln_words[:, half, :, :].rearrange("p c w -> p (c w)").bitcast(FP8X4),
-                scales=ln_scales[:, half, :, :].rearrange("p c w -> p (c w)"),
-                in_=ln_grouped[:, half, :, :, :].rearrange("p c w t -> p (c w t)"),
-            )
-
-        h_words = keep.tile([P, HALVES, F1_PASSES, HALF], U32, align_bytes=64)
-        h_scales = keep.tile([P, HALVES, F1_PASSES, HALF], U8, align_bytes=64)
-
-        def fc1_unit(half, pair):
-            pre_tiles = []
-            for gl in range(PAIR):
-                g = pair * PAIR + gl
-                cols = slice(g * K_PASS, (g + 1) * K_PASS)
-                for il in range(HALF_TILES):
-                    toks = slice(il * P, (il + 1) * P)
-                    acc = psum.tile([P, N_TILE], F32, tag="bank", name="fc1_acc")
-                    for c in range(D_PASSES):
-                        nc.tensor.matmul_mx(
-                            out=acc[:],
-                            lhsT=ln_words[:, half, c, toks].bitcast(FP8X4),
-                            lhsT_scale=ln_scales[:, half, c, toks],
-                            rhs=w1_words[:, c, cols].bitcast(FP8X4),
-                            rhs_scale=w1_planes[4 * c : P, cols],
-                            start=(c == 0),
-                            stop=(c == D_PASSES - 1),
-                        )
-                    pre = work.tile([P, PACK, P], F32, tag="pre", bufs=12, name="pre")
-                    nc.vector.tensor_tensor(
-                        out=pre[:].rearrange("p t q -> p q t"),
-                        in0=acc[:].rearrange("p (q t) -> p q t", t=PACK),
-                        in1=b1_bc[:, cols].rearrange("p (q t) -> p q t", t=PACK),
-                        op=ALU.add,
+                    nc.tensor.transpose(
+                        ln_banks[c * PACK + t][:, i * P : (i + 1) * P], xhat[:, i, c, t, :], ident[:]
                     )
-                    pre_tiles.append(pre)
-            return pre_tiles
 
-        def gelu_unit(pre_tiles):
-            h_grouped = work.tile(
-                [P, PAIR * HALF_TILES, P, PACK], BF16, tag="h_grouped", bufs=3, align_bytes=64, name="h_grouped"
+        for i in range(TOK_TILES + 1):
+            if i < TOK_TILES:
+                statistics(i)
+            if i > 0:
+                normalise_and_turn(i - 1)
+
+        ln_planes = keep.tile([P, D_PASSES, PACK, T], BF16)
+        ln_grouped = keep.tile([P, D_PASSES, T, PACK], BF16, align_bytes=64)
+        ln_words = keep.tile([P, D_PASSES, T], U32, align_bytes=64)
+        ln_scales = keep.tile([P, D_PASSES, T], U8, align_bytes=64)
+        for c in range(D_PASSES):
+            for t in range(PACK):
+                if t % 2 == 0:
+                    nc.scalar.activation(
+                        out=ln_planes[:, c, t, :],
+                        in_=ln_banks[c * PACK + t][:],
+                        func=ACT.Identity,
+                        bias=beta_f[:, c, t : t + 1],
+                        scale=gamma_f[:, c, t : t + 1],
+                    )
+                else:
+                    nc.vector.tensor_scalar(
+                        out=ln_planes[:, c, t, :],
+                        in0=ln_banks[c * PACK + t][:],
+                        scalar1=gamma_f[:, c, t : t + 1],
+                        scalar2=beta_f[:, c, t : t + 1],
+                        op0=ALU.mult,
+                        op1=ALU.add,
+                    )
+            nc.vector.tensor_copy(
+                out=ln_grouped[:, c, :, :].rearrange("p (a b) t -> p a t b", b=4),
+                in_=ln_planes[:, c, :, :].rearrange("p t (a b) -> p a t b", b=4),
             )
-            for k in range(PAIR * HALF_TILES):
-                turned = psum.tile([P, PACK, P], F32, tag="bank", name="turned")
-                for t in range(PACK):
-                    nc.tensor.transpose(turned[:, t, :], pre_tiles[k][:, t, :], ident[:])
-                nc.scalar.activation(
-                    out=h_grouped[:, k, :, :],
-                    in_=turned[:].rearrange("p t w -> p w t"),
-                    func=ACT.Gelu_apprx_tanh,
-                )
-            return h_grouped
-
-        def quantise_unit(half, pair, h_grouped):
-            groups = slice(pair * PAIR, (pair + 1) * PAIR)
+        for c in range(D_PASSES):
             nc.vector.quantize_mx(
-                out=h_words[:, half, groups, :].rearrange("p g w -> p (g w)").bitcast(FP8X4),
-                scales=h_scales[:, half, groups, :].rearrange("p g w -> p (g w)"),
-                in_=h_grouped[:].rearrange("p k w t -> p (k w t)"),
+                out=ln_words[:, c, :].bitcast(FP8X4),
+                scales=ln_scales[:, c, :],
+                in_=ln_grouped[:, c, :, :].rearrange("p w t -> p (w t)"),
             )
 
-        for il in range(HALF_TILES):
-            statistics(0, il)
-            normalise(0, il)
-        for il in range(HALF_TILES):
-            statistics(1, il)
-        turn_ln(0)
-        quantise_ln(0)
-        for il in range(HALF_TILES):
-            normalise(1, il)
+        park = out.bitcast(BF16).rearrange("r (a w) -> (r a) w", w=T)
+        h_words = keep.tile([P, F1_PASSES, T], U32, align_bytes=64)
+        h_scales = keep.tile([P, F1_PASSES, T], U8, align_bytes=64)
 
-        units = [(half, pair) for half in range(HALVES) for pair in range(PAIRS)]
-        pre_of = {0: fc1_unit(0, 0)}
-        h_of = {}
-        for u in range(len(units)):
-            if u + 1 < len(units):
-                pre_of[u + 1] = fc1_unit(units[u + 1][0], units[u + 1][1])
-            h_of[u] = gelu_unit(pre_of[u])
-            if u == 0:
-                turn_ln(1)
-            if u == 1:
-                quantise_ln(1)
-            if u > 0:
-                quantise_unit(units[u - 1][0], units[u - 1][1], h_of[u - 1])
-        last = len(units) - 1
-        quantise_unit(units[last][0], units[last][1], h_of[last])
+        def parked_rows(g):
+            return park[(g % PARKED) * K_PASS : (g % PARKED + 1) * K_PASS, :]
 
-        for half in range(HALVES):
-            for il in range(HALF_TILES):
-                toks = slice(il * P, (il + 1) * P)
-                row = (half * HALF_TILES + il) * P
-                for j in range(F2_TILES):
-                    cols = slice(j * N_TILE, (j + 1) * N_TILE)
-                    acc2 = psum.tile([P, N_TILE], F32, tag="bank", name="fc2_acc")
-                    for g in range(F1_PASSES):
-                        nc.tensor.matmul_mx(
-                            out=acc2[:],
-                            lhsT=h_words[:, half, g, toks].bitcast(FP8X4),
-                            lhsT_scale=h_scales[:, half, g, toks],
-                            rhs=w2_words[:, g, cols].bitcast(FP8X4),
-                            rhs_scale=w2_planes[4 * (g % 4) : P, g // 4, cols],
-                            start=(g == 0),
-                            stop=(g == F1_PASSES - 1),
-                        )
-                    res = work.tile([P, N_TILE], F32, tag="res", bufs=4, name="res")
-                    nc.vector.tensor_tensor(out=res[:], in0=acc2[:], in1=b2_bc[:, cols], op=ALU.add)
-                    nc.sync.dma_start(out=out[row : row + P, cols], in_=res[:])
+        def fc1_group(g):
+            h_cols = work.tile([P, PACK, T], BF16, tag="h_cols", bufs=3, name="h_cols")
+            for jl in range(PACK):
+                j = g * PACK + jl
+                cols = slice(j * P, (j + 1) * P)
+                acc = psum.tile([P, T], F32, tag="short", name="fc1_acc")
+                for c in range(D_PASSES):
+                    nc.tensor.matmul_mx(
+                        out=acc[:],
+                        lhsT=w1_words[:, c, cols].bitcast(FP8X4),
+                        lhsT_scale=w1_planes[4 * c : P, cols],
+                        rhs=ln_words[:, c, :].bitcast(FP8X4),
+                        rhs_scale=ln_scales[:, c, :],
+                        start=(c == 0),
+                        stop=(c == D_PASSES - 1),
+                    )
+                nc.scalar.activation(
+                    out=h_cols[:, jl, :],
+                    in_=acc[:],
+                    func=ACT.Gelu_apprx_tanh,
+                    bias=b1_col[:, j : j + 1],
+                    scale=1.0,
+                )
+            nc.sync.dma_start(out=parked_rows(g).rearrange("(jl m) w -> m jl w", m=P), in_=h_cols[:])
+
+        def fetch_group(g):
+            h_rows = work.tile([P, PACK, T], BF16, tag="h_rows", bufs=LAG + 1, name="h_rows")
+            nc.sync.dma_start(out=h_rows[:], in_=parked_rows(g).rearrange("(q t) w -> q t w", t=PACK))
+            return h_rows
+
+        def quantise_group(g, h_rows):
+            h_grouped = work.tile([P, T, PACK], BF16, tag="h_grouped", bufs=2, align_bytes=64, name="h_grouped")
+            nc.vector.tensor_copy(
+                out=h_grouped[:].rearrange("p (a b) t -> p a t b", b=4),
+                in_=h_rows[:].rearrange("p t (a b) -> p a t b", b=4),
+            )
+            nc.vector.quantize_mx(
+                out=h_words[:, g, :].bitcast(FP8X4),
+                scales=h_scales[:, g, :],
+                in_=h_grouped[:].rearrange("p w t -> p (w t)"),
+            )
+
+        def fc2_pass(g, i, j, acc):
+            toks = slice(i * P, (i + 1) * P)
+            cols = slice(j * N_TILE, (j + 1) * N_TILE)
+            nc.tensor.matmul_mx(
+                out=acc[:],
+                lhsT=h_words[:, g, toks].bitcast(FP8X4),
+                lhsT_scale=h_scales[:, g, toks],
+                rhs=w2_words[:, g, cols].bitcast(FP8X4),
+                rhs_scale=w2_planes[4 * (g % 4) : P, g // 4, cols],
+                start=(g == 0),
+                stop=(g == F1_PASSES - 1),
+            )
+
+        def finish_bank(i, j, acc):
+            cols = slice(j * N_TILE, (j + 1) * N_TILE)
+            res = work.tile([P, N_TILE], F32, tag="res", bufs=4, name="res")
+            nc.vector.tensor_tensor(out=res[:], in0=acc[:], in1=b2_bc[:, cols], op=ALU.add)
+            nc.sync.dma_start(out=out[i * P : (i + 1) * P, cols], in_=res[:])
+
+        h_rows_of = {}
+        accs0 = [psum.tile([P, N_TILE], F32, tag="long", name="fc2_acc0_%d" % i) for i in range(TOK_TILES)]
+        accs1 = []
+        for s in range(F1_PASSES + LAG):
+            if s < F1_PASSES:
+                fc1_group(s)
+            if 0 < s <= F1_PASSES:
+                h_rows_of[s - 1] = fetch_group(s - 1)
+            if s == F1_PASSES:
+                accs1.extend(
+                    psum.tile([P, N_TILE], F32, tag="short", name="fc2_acc1_%d" % i) for i in range(TOK_TILES)
+                )
+            if s >= F1_PASSES:
+                for i in range(TOK_TILES):
+                    fc2_pass(s - F1_PASSES, i, 1, accs1[i])
+            if s >= LAG:
+                quantise_group(s - LAG, h_rows_of[s - LAG])
+                for i in range(TOK_TILES):
+                    fc2_pass(s - LAG, i, 0, accs0[i])
+        for i in range(TOK_TILES):
+            finish_bank(i, 0, accs0[i])
+        for i in range(TOK_TILES):
+            for g in range(LAG, F1_PASSES):
+                fc2_pass(g, i, 1, accs1[i])
+            finish_bank(i, 1, accs1[i])

@@ -26,7 +26,8 @@ F1_TILES = F1 // P
 F2_TILES = F2 // N_TILE
 W1_CHUNK = 1024
 PARKED = 4
-LAG = 4
+LAG = 5
+W2_AHEAD = 5
 
 FLOPS = 2 * T * D * F1 + 2 * T * F1 * F2
 
@@ -94,13 +95,16 @@ def tile_layernormmlp_kernel(
                     in_=fc2_kernel_scales[4 * four : 4 * four + 4, 4 * quad : 4 * quad + 4, :].bitcast(I32),
                 )
         w2_words = keep.tile([P, F1_PASSES, F2], U32, align_bytes=64)
-        for g in range(F1_PASSES):
+
+        def load_w2(g):
             nc.sync.dma_start(
                 out=w2_words[:, g, :].bitcast(I32),
                 in_=fc2_kernel_words[g].rearrange("p n t -> p (n t)").bitcast(I32),
             )
+
+        for g in range(W2_AHEAD):
+            load_w2(g)
         b2_bc = keep.tile([P, F2], BF16)
-        nc.sync.dma_start(out=b2_bc[:], in_=fc2_bias.partition_broadcast(P))
 
         gamma_f = keep.tile([P, D_PASSES, PACK], F32)
         beta_f = keep.tile([P, D_PASSES, PACK], F32)
@@ -208,10 +212,11 @@ def tile_layernormmlp_kernel(
 
         def fc1_group(g):
             h_cols = work.tile([P, PACK, T], BF16, tag="h_cols", bufs=3, name="h_cols")
+            fc1_tag = "long" if (g < LAG and g % 2 == 1) else "short"
             for jl in range(PACK):
                 j = g * PACK + jl
                 cols = slice(j * P, (j + 1) * P)
-                acc = psum.tile([P, T], F32, tag="short", name="fc1_acc")
+                acc = psum.tile([P, T], F32, tag=fc1_tag, name="fc1_acc")
                 for c in range(D_PASSES):
                     nc.tensor.matmul_mx(
                         out=acc[:],
@@ -268,20 +273,27 @@ def tile_layernormmlp_kernel(
             nc.sync.dma_start(out=out[i * P : (i + 1) * P, cols], in_=res[:])
 
         h_rows_of = {}
-        accs0 = [psum.tile([P, N_TILE], F32, tag="long", name="fc2_acc0_%d" % i) for i in range(TOK_TILES)]
+        accs0 = []
         accs1 = []
         for s in range(F1_PASSES + LAG):
             if s < F1_PASSES:
                 fc1_group(s)
             if 0 < s <= F1_PASSES:
                 h_rows_of[s - 1] = fetch_group(s - 1)
+            if W2_AHEAD + s < F1_PASSES:
+                load_w2(W2_AHEAD + s)
             if s == F1_PASSES:
+                nc.sync.dma_start(out=b2_bc[:], in_=fc2_bias.partition_broadcast(P))
                 accs1.extend(
                     psum.tile([P, N_TILE], F32, tag="short", name="fc2_acc1_%d" % i) for i in range(TOK_TILES)
                 )
             if s >= F1_PASSES:
                 for i in range(TOK_TILES):
                     fc2_pass(s - F1_PASSES, i, 1, accs1[i])
+            if s == LAG:
+                accs0.extend(
+                    psum.tile([P, N_TILE], F32, tag="long", name="fc2_acc0_%d" % i) for i in range(TOK_TILES)
+                )
             if s >= LAG:
                 quantise_group(s - LAG, h_rows_of[s - LAG])
                 for i in range(TOK_TILES):

@@ -20,6 +20,7 @@ N_TILE = 512
 T, D, F1, F2 = 512, 1024, 4096, 1024
 EPS = 1e-3
 TOK_TILES = T // P
+HALF = T // 2
 D_PASSES = D // K_PASS
 F1_PASSES = F1 // K_PASS
 F1_TILES = F1 // P
@@ -124,14 +125,17 @@ def tile_layernormmlp_kernel(
         shift = keep.tile([P, TOK_TILES], F32)
         xhat = keep.tile([P, TOK_TILES, D_PASSES, PACK, P], F32)
         ln_banks = [
-            psum.tile([P, T], F32, tag=("short" if k < PACK else "long"), name="ln_bank%d" % k)
-            for k in range(D_PASSES * PACK)
+            [
+                psum.tile([P, 2, HALF], F32, tag=("short" if half == 0 else "long"), name="ln_bank%d_%d" % (half, k))
+                for k in range(D_PASSES * PACK // 2)
+            ]
+            for half in range(2)
         ]
 
         def statistics(i):
-            for half in range(2):
+            for part in range(2):
                 nc.vector.bn_stats(
-                    out=stats[:, i, half, :], in_=x_sb[:, i, half * 512 : (half + 1) * 512]
+                    out=stats[:, i, part, :], in_=x_sb[:, i, part * 512 : (part + 1) * 512]
                 )
             nc.vector.bn_aggr(
                 out=mean_var[:, i, :], in_=stats[:, i, :, :].rearrange("p h s -> p (h s)")
@@ -157,11 +161,11 @@ def tile_layernormmlp_kernel(
                 bias=shift[:, i : i + 1],
                 scale=rstd[:, i : i + 1],
             )
-            for c in range(D_PASSES):
-                for t in range(PACK):
-                    nc.tensor.transpose(
-                        ln_banks[c * PACK + t][:, i * P : (i + 1) * P], xhat[:, i, c, t, :], ident[:]
-                    )
+            toks = slice((i % 2) * P, (i % 2 + 1) * P)
+            for k in range(D_PASSES * PACK):
+                nc.tensor.transpose(
+                    ln_banks[i // 2][k // 2][:, k % 2, toks], xhat[:, i, k // PACK, k % PACK, :], ident[:]
+                )
 
         for i in range(TOK_TILES + 1):
             if i < TOK_TILES:
@@ -173,35 +177,45 @@ def tile_layernormmlp_kernel(
         ln_grouped = keep.tile([P, D_PASSES, T, PACK], BF16, align_bytes=64)
         ln_words = keep.tile([P, D_PASSES, T], U32, align_bytes=64)
         ln_scales = keep.tile([P, D_PASSES, T], U8, align_bytes=64)
-        for c in range(D_PASSES):
-            for t in range(PACK):
-                if t % 2 == 0:
-                    nc.scalar.activation(
-                        out=ln_planes[:, c, t, :],
-                        in_=ln_banks[c * PACK + t][:],
-                        func=ACT.Identity,
-                        bias=beta_f[:, c, t : t + 1],
-                        scale=gamma_f[:, c, t : t + 1],
-                    )
-                else:
-                    nc.vector.tensor_scalar(
-                        out=ln_planes[:, c, t, :],
-                        in0=ln_banks[c * PACK + t][:],
-                        scalar1=gamma_f[:, c, t : t + 1],
-                        scalar2=beta_f[:, c, t : t + 1],
-                        op0=ALU.mult,
-                        op1=ALU.add,
-                    )
+
+        def regroup_ln(half, c):
+            toks = slice(half * HALF, (half + 1) * HALF)
             nc.vector.tensor_copy(
-                out=ln_grouped[:, c, :, :].rearrange("p (a b) t -> p a t b", b=4),
-                in_=ln_planes[:, c, :, :].rearrange("p t (a b) -> p a t b", b=4),
+                out=ln_grouped[:, c, toks, :].rearrange("p (a b) t -> p a t b", b=4),
+                in_=ln_planes[:, c, :, toks].rearrange("p t (a b) -> p a t b", b=4),
+            )
+
+        def quantise_ln(half, c):
+            toks = slice(half * HALF, (half + 1) * HALF)
+            nc.vector.quantize_mx(
+                out=ln_words[:, c, toks].bitcast(FP8X4),
+                scales=ln_scales[:, c, toks],
+                in_=ln_grouped[:, c, toks, :].rearrange("p w t -> p (w t)"),
+            )
+
+        for k in range(D_PASSES * PACK):
+            nc.vector.tensor_scalar(
+                out=ln_planes[:, k // PACK, k % PACK, 0:HALF],
+                in0=ln_banks[0][k // 2][:, k % 2, :],
+                scalar1=gamma_f[:, k // PACK, k % PACK : k % PACK + 1],
+                scalar2=beta_f[:, k // PACK, k % PACK : k % PACK + 1],
+                op0=ALU.mult,
+                op1=ALU.add,
+            )
+            nc.scalar.activation(
+                out=ln_planes[:, k // PACK, k % PACK, HALF:T],
+                in_=ln_banks[1][k // 2][:, k % 2, :],
+                func=ACT.Identity,
+                bias=beta_f[:, k // PACK, k % PACK : k % PACK + 1],
+                scale=gamma_f[:, k // PACK, k % PACK : k % PACK + 1],
             )
         for c in range(D_PASSES):
-            nc.vector.quantize_mx(
-                out=ln_words[:, c, :].bitcast(FP8X4),
-                scales=ln_scales[:, c, :],
-                in_=ln_grouped[:, c, :, :].rearrange("p w t -> p (w t)"),
-            )
+            regroup_ln(0, c)
+        for c in range(D_PASSES):
+            quantise_ln(0, c)
+        for c in range(D_PASSES):
+            regroup_ln(1, c)
+            quantise_ln(1, c)
 
         park = out.bitcast(BF16).rearrange("r (a w) -> (r a) w", w=T)
         h_words = keep.tile([P, F1_PASSES, T], U32, align_bytes=64)
@@ -211,7 +225,7 @@ def tile_layernormmlp_kernel(
             return park[(g % PARKED) * K_PASS : (g % PARKED + 1) * K_PASS, :]
 
         def fc1_group(g):
-            h_cols = work.tile([P, PACK, T], BF16, tag="h_cols", bufs=3, name="h_cols")
+            h_cols = work.tile([P, PACK, T], BF16, tag="h_cols", bufs=4, name="h_cols")
             fc1_tag = "long" if (g < LAG and g % 2 == 1) else "short"
             for jl in range(PACK):
                 j = g * PACK + jl

@@ -107,31 +107,12 @@ def tile_layernormmlp_kernel(
             load_w2(g)
         b2_bc = keep.tile([P, F2], BF16)
 
-        gamma_f = keep.tile([P, D_PASSES, PACK], F32)
-        beta_f = keep.tile([P, D_PASSES, PACK], F32)
-        nc.vector.tensor_copy(out=gamma_f[:], in_=gamma_bf[:])
-        nc.vector.tensor_copy(out=beta_f[:], in_=beta_bf[:])
-        b1_rows_f = keep.tile([P, P], F32)
-        nc.vector.tensor_copy(out=b1_rows_f[:], in_=b1_rows[:])
-        b1_bank = psum.tile([P, P], F32, tag="short", name="b1_bank")
-        nc.tensor.transpose(b1_bank[:], b1_rows_f[:], ident[:])
-        b1_col = keep.tile([P, F1_TILES], F32)
-        nc.vector.tensor_copy(out=b1_col[:], in_=b1_bank[:, 0:F1_TILES])
-
         stats = keep.tile([P, TOK_TILES, 2, 6], F32)
         mean_var = keep.tile([P, TOK_TILES, 2], F32)
         std = keep.tile([P, TOK_TILES], F32)
         rstd = keep.tile([P, TOK_TILES], F32)
         shift = keep.tile([P, TOK_TILES], F32)
         xhat = keep.tile([P, TOK_TILES, D_PASSES, PACK, P], F32)
-        ln_banks = [
-            [
-                psum.tile([P, 2, HALF], F32, tag=("short" if half == 0 else "long"), name="ln_bank%d_%d" % (half, k))
-                for k in range(D_PASSES * PACK // 2)
-            ]
-            for half in range(2)
-        ]
-
         def statistics(i):
             for part in range(2):
                 nc.vector.bn_stats(
@@ -167,11 +148,31 @@ def tile_layernormmlp_kernel(
                     ln_banks[i // 2][k // 2][:, k % 2, toks], xhat[:, i, k // PACK, k % PACK, :], ident[:]
                 )
 
-        for i in range(TOK_TILES + 1):
+        statistics(0)
+        statistics(1)
+        gamma_f = keep.tile([P, D_PASSES, PACK], F32)
+        beta_f = keep.tile([P, D_PASSES, PACK], F32)
+        nc.vector.tensor_copy(out=gamma_f[:], in_=gamma_bf[:])
+        nc.vector.tensor_copy(out=beta_f[:], in_=beta_bf[:])
+        b1_rows_f = keep.tile([P, P], F32)
+        nc.vector.tensor_copy(out=b1_rows_f[:], in_=b1_rows[:])
+        b1_bank = psum.tile([P, P], F32, tag="short", name="b1_bank")
+        nc.tensor.transpose(b1_bank[:], b1_rows_f[:], ident[:])
+        b1_col = keep.tile([P, F1_TILES], F32)
+        nc.vector.tensor_copy(out=b1_col[:], in_=b1_bank[:, 0:F1_TILES])
+
+        ln_banks = [
+            [
+                psum.tile([P, 2, HALF], F32, tag=("short" if half == 0 else "long"), name="ln_bank%d_%d" % (half, k))
+                for k in range(D_PASSES * PACK // 2)
+            ]
+            for half in range(2)
+        ]
+
+        for i in range(2, TOK_TILES + 2):
+            normalise_and_turn(i - 2)
             if i < TOK_TILES:
                 statistics(i)
-            if i > 0:
-                normalise_and_turn(i - 1)
 
         ln_planes = keep.tile([P, D_PASSES, PACK, T], BF16)
         ln_grouped = keep.tile([P, D_PASSES, T, PACK], BF16, align_bytes=64)

@@ -21,14 +21,20 @@ T, D, F1, F2 = 512, 1024, 4096, 1024
 EPS = 1e-3
 TOK_TILES = T // P
 HALF = T // 2
+HALF_TILES = HALF // P
 D_PASSES = D // K_PASS
+PLANES = D_PASSES * PACK
 F1_PASSES = F1 // K_PASS
 F1_TILES = F1 // P
 F2_TILES = F2 // N_TILE
 W1_CHUNK = 1024
-PARKED = 4
-LAG = 5
-W2_AHEAD = 5
+PAIR = 2
+PAIRS = F1_PASSES // PAIR
+W2_AHEAD = 1
+TURN_AFTER = 3
+PHASE1_LOADS = ((1,), (2, 3), (4,), (5,))
+G_MAJOR = 4
+WOVEN = {3: 0, 4: 1, 6: 2}
 
 FLOPS = 2 * T * D * F1 + 2 * T * F1 * F2
 
@@ -53,14 +59,16 @@ def tile_layernormmlp_kernel(
         psum = ctx.enter_context(tc.psum_pool(name="psum", bufs=4))
         ctx.enter_context(tc.manual_schedule())
 
+        zero_col = keep.tile([P, 1], F32)
+        nc.vector.memset(zero_col[:], 0.0)
         w1_planes = keep.tile([P, F1], U8, align_bytes=64)
         w2_planes = keep.tile([P, F1_PASSES // 4, F2], U8, align_bytes=64)
         nc.vector.memset(w1_planes[:].bitcast(I32), 0)
-        nc.vector.memset(w2_planes[:].rearrange("p a n -> p (a n)").bitcast(I32), 0)
-        eps = keep.tile([P, 1], F32)
-        nc.vector.memset(eps[:], EPS)
         b1_rows = keep.tile([P, P], BF16)
         nc.vector.memset(b1_rows[:], 0.0)
+        minus_half = keep.tile([P, 1], F32)
+        nc.vector.memset(minus_half[:], -0.5)
+        nc.vector.memset(w2_planes[:].rearrange("p a n -> p (a n)").bitcast(I32), 0)
         ident = keep.tile([P, P], F32)
         make_identity(nc, ident[:])
 
@@ -70,15 +78,18 @@ def tile_layernormmlp_kernel(
 
         gamma_bf = keep.tile([P, D_PASSES, PACK], BF16)
         beta_bf = keep.tile([P, D_PASSES, PACK], BF16)
+        nc.scalar.dma_start(out=b1_rows[0:F1_TILES, :], in_=fc1_bias.rearrange("(j m) -> j m", m=P))
         nc.scalar.dma_start(out=gamma_bf[:], in_=gamma.rearrange("(c p t) -> p c t", p=P, t=PACK))
         nc.scalar.dma_start(out=beta_bf[:], in_=beta.rearrange("(c p t) -> p c t", p=P, t=PACK))
-        nc.scalar.dma_start(out=b1_rows[0:F1_TILES, :], in_=fc1_bias.rearrange("(j m) -> j m", m=P))
+        warm = keep.tile([P, 1], F32)
+        nc.scalar.activation(out=warm[:], in_=zero_col[:], func=ACT.Gelu_apprx_tanh, bias=0.0, scale=1.0)
 
         for quad in range(4):
             nc.sync.dma_start(
                 out=w1_planes[32 * quad : 32 * quad + 4 * D_PASSES, :].bitcast(I32),
                 in_=fc1_kernel_scales[:, 4 * quad : 4 * quad + 4, :].bitcast(I32),
             )
+        w1p_planes = keep.tile([P, F1], U8, align_bytes=64)
         w1_words = keep.tile([P, D_PASSES, F1], U32, align_bytes=64)
         for chunk in range(F1 // W1_CHUNK):
             cols = slice(chunk * W1_CHUNK, (chunk + 1) * W1_CHUNK)
@@ -109,24 +120,36 @@ def tile_layernormmlp_kernel(
 
         stats = keep.tile([P, TOK_TILES, 2, 6], F32)
         mean_var = keep.tile([P, TOK_TILES, 2], F32)
-        std = keep.tile([P, TOK_TILES], F32)
+        var_eps = keep.tile([P, TOK_TILES], F32)
         rstd = keep.tile([P, TOK_TILES], F32)
         shift = keep.tile([P, TOK_TILES], F32)
-        xhat = keep.tile([P, TOK_TILES, D_PASSES, PACK, P], F32)
-        def statistics(i):
-            for part in range(2):
-                nc.vector.bn_stats(
-                    out=stats[:, i, part, :], in_=x_sb[:, i, part * 512 : (part + 1) * 512]
-                )
+        xhat = work.tile([P, TOK_TILES, D_PASSES, PACK, P], F32, tag="big", bufs=2, align_bytes=64, name="xhat")
+        b1p = keep.tile([P, F1_PASSES, PACK], BF16)
+        gamma_f = keep.tile([P, D_PASSES, PACK], F32)
+        beta_f = keep.tile([P, D_PASSES, PACK], F32)
+        b1_rows_f = keep.tile([P, P], F32)
+        b1_col = keep.tile([P, F1_TILES], F32)
+        ln_planes = keep.tile([P, D_PASSES, PACK, T], BF16)
+        ln_grouped = keep.tile([P, D_PASSES, T, PACK], BF16, align_bytes=64)
+        ln_words = keep.tile([P, D_PASSES, T], U32, align_bytes=64)
+        ln_scales = keep.tile([P, D_PASSES, T], U8, align_bytes=64)
+
+        def first_statistics(i):
+            nc.vector.bn_stats(out=stats[:, i, 0, :], in_=x_sb[:, i, 0:512])
+
+        def last_statistics(i):
+            nc.vector.bn_stats(out=stats[:, i, 1, :], in_=x_sb[:, i, 512:1024])
             nc.vector.bn_aggr(
                 out=mean_var[:, i, :], in_=stats[:, i, :, :].rearrange("p h s -> p (h s)")
             )
-            nc.scalar.activation(
-                out=std[:, i : i + 1], in_=mean_var[:, i, 1:2], func=ACT.Sqrt, bias=eps[:, 0:1], scale=1.0
+            nc.vector.tensor_scalar(
+                out=var_eps[:, i : i + 1], in0=mean_var[:, i, 1:2], scalar1=EPS, scalar2=None, op0=ALU.add
+            )
+            nc.gpsimd.tensor_tensor(
+                out=rstd[:, i : i + 1], in0=var_eps[:, i : i + 1], in1=minus_half[:], op=ALU.pow
             )
 
-        def normalise_and_turn(i):
-            nc.vector.reciprocal(out=rstd[:, i : i + 1], in_=std[:, i : i + 1])
+        def shift_of(i):
             nc.vector.scalar_tensor_tensor(
                 out=shift[:, i : i + 1],
                 in0=mean_var[:, i, 0:1],
@@ -135,49 +158,49 @@ def tile_layernormmlp_kernel(
                 op0=ALU.mult,
                 op1=ALU.mult,
             )
+
+        def normalise_on_scalar(i, c):
             nc.scalar.activation(
-                out=xhat[:, i, :, :, :].rearrange("p c t q -> p c q t"),
-                in_=x_sb[:, i, :].rearrange("p (c q t) -> p c q t", c=D_PASSES, t=PACK),
+                out=xhat[:, i, c, :, :].rearrange("p t q -> p q t"),
+                in_=x_sb[:, i, c * K_PASS : (c + 1) * K_PASS].rearrange("p (q t) -> p q t", t=PACK),
                 func=ACT.Identity,
                 bias=shift[:, i : i + 1],
                 scale=rstd[:, i : i + 1],
             )
-            toks = slice((i % 2) * P, (i % 2 + 1) * P)
-            for k in range(D_PASSES * PACK):
-                nc.tensor.transpose(
-                    ln_banks[i // 2][k // 2][:, k % 2, toks], xhat[:, i, k // PACK, k % PACK, :], ident[:]
-                )
 
-        statistics(0)
-        statistics(1)
-        gamma_f = keep.tile([P, D_PASSES, PACK], F32)
-        beta_f = keep.tile([P, D_PASSES, PACK], F32)
-        nc.vector.tensor_copy(out=gamma_f[:], in_=gamma_bf[:])
-        nc.vector.tensor_copy(out=beta_f[:], in_=beta_bf[:])
-        b1_rows_f = keep.tile([P, P], F32)
-        nc.vector.tensor_copy(out=b1_rows_f[:], in_=b1_rows[:])
-        b1_bank = psum.tile([P, P], F32, tag="short", name="b1_bank")
-        nc.tensor.transpose(b1_bank[:], b1_rows_f[:], ident[:])
-        b1_col = keep.tile([P, F1_TILES], F32)
-        nc.vector.tensor_copy(out=b1_col[:], in_=b1_bank[:, 0:F1_TILES])
+        def normalise_on_vector(i, c):
+            nc.vector.tensor_scalar(
+                out=xhat[:, i, c, :, :].rearrange("p t q -> p q t"),
+                in0=x_sb[:, i, c * K_PASS : (c + 1) * K_PASS].rearrange("p (q t) -> p q t", t=PACK),
+                scalar1=mean_var[:, i, 0:1],
+                scalar2=rstd[:, i : i + 1],
+                op0=ALU.subtract,
+                op1=ALU.mult,
+            )
 
-        ln_banks = [
-            [
-                psum.tile([P, 2, HALF], F32, tag=("short" if half == 0 else "long"), name="ln_bank%d_%d" % (half, k))
-                for k in range(D_PASSES * PACK // 2)
-            ]
-            for half in range(2)
-        ]
+        def turn(i, c, banks):
+            toks = slice((i % HALF_TILES) * P, (i % HALF_TILES + 1) * P)
+            for k in range(c * PACK, (c + 1) * PACK):
+                nc.tensor.transpose(banks[k // 2][:, k % 2, toks], xhat[:, i, k // PACK, k % PACK, :], ident[:])
 
-        for i in range(2, TOK_TILES + 2):
-            normalise_and_turn(i - 2)
-            if i < TOK_TILES:
-                statistics(i)
+        def leave_on_vector(half, k, banks):
+            nc.vector.tensor_scalar(
+                out=ln_planes[:, k // PACK, k % PACK, half * HALF : (half + 1) * HALF],
+                in0=banks[k // 2][:, k % 2, :],
+                scalar1=gamma_f[:, k // PACK, k % PACK : k % PACK + 1],
+                scalar2=beta_f[:, k // PACK, k % PACK : k % PACK + 1],
+                op0=ALU.mult,
+                op1=ALU.add,
+            )
 
-        ln_planes = keep.tile([P, D_PASSES, PACK, T], BF16)
-        ln_grouped = keep.tile([P, D_PASSES, T, PACK], BF16, align_bytes=64)
-        ln_words = keep.tile([P, D_PASSES, T], U32, align_bytes=64)
-        ln_scales = keep.tile([P, D_PASSES, T], U8, align_bytes=64)
+        def leave_on_scalar(half, k, banks):
+            nc.scalar.activation(
+                out=ln_planes[:, k // PACK, k % PACK, half * HALF : (half + 1) * HALF],
+                in_=banks[k // 2][:, k % 2, :],
+                func=ACT.Identity,
+                bias=beta_f[:, k // PACK, k % PACK : k % PACK + 1],
+                scale=gamma_f[:, k // PACK, k % PACK : k % PACK + 1],
+            )
 
         def regroup_ln(half, c):
             toks = slice(half * HALF, (half + 1) * HALF)
@@ -194,128 +217,228 @@ def tile_layernormmlp_kernel(
                 in_=ln_grouped[:, c, toks, :].rearrange("p w t -> p (w t)"),
             )
 
-        for k in range(D_PASSES * PACK):
-            nc.vector.tensor_scalar(
-                out=ln_planes[:, k // PACK, k % PACK, 0:HALF],
-                in0=ln_banks[0][k // 2][:, k % 2, :],
-                scalar1=gamma_f[:, k // PACK, k % PACK : k % PACK + 1],
-                scalar2=beta_f[:, k // PACK, k % PACK : k % PACK + 1],
-                op0=ALU.mult,
-                op1=ALU.add,
+        first_statistics(0)
+        last_statistics(0)
+        nc.gpsimd.tensor_copy(out=b1_rows_f[:], in_=b1_rows[:])
+        nc.gpsimd.tensor_copy(out=gamma_f[:], in_=gamma_bf[:])
+        nc.gpsimd.tensor_copy(out=beta_f[:], in_=beta_bf[:])
+        first_statistics(1)
+        shift_of(0)
+        last_statistics(1)
+        b1_bank = psum.tile([P, P], F32, tag="short", name="b1_bank")
+        nc.tensor.transpose(b1_bank[:], b1_rows_f[:], ident[:])
+        ln_banks0 = [psum.tile([P, 2, HALF], F32, tag="short", name="ln_bank0_%d" % b) for b in range(PLANES // 2)]
+        for c in range(D_PASSES):
+            normalise_on_scalar(0, c)
+            turn(0, c, ln_banks0)
+        nc.scalar.activation(out=b1_col[:], in_=b1_bank[:, 0:F1_TILES], func=ACT.Identity, bias=0.0, scale=1.0)
+        nc.scalar.dma_start(out=b1p[:], in_=fc1_bias.rearrange("(g p t) -> p g t", p=P, t=PACK))
+        first_statistics(2)
+        for c in range(D_PASSES):
+            normalise_on_vector(1, c)
+            turn(1, c, ln_banks0)
+        leave_on_scalar(0, 0, ln_banks0)
+        leave_on_scalar(0, 1, ln_banks0)
+        leave_on_vector(0, 2, ln_banks0)
+        leave_on_vector(0, 3, ln_banks0)
+        for k in range(PACK, PLANES):
+            leave_on_scalar(0, k, ln_banks0)
+        regroup_ln(0, 0)
+        quantise_ln(0, 0)
+        regroup_ln(0, 1)
+        quantise_ln(0, 1)
+        last_statistics(2)
+        first_statistics(3)
+        last_statistics(3)
+        for t in range(PACK):
+            nc.gpsimd.tensor_copy(
+                out=w1p_planes[:].rearrange("p (g t m) -> p t g m", t=PACK, m=P)[:, t, :, :],
+                in_=w1_planes[:].rearrange("p (g m t) -> p t g m", m=P, t=PACK)[:, t, :, :],
             )
-            nc.scalar.activation(
-                out=ln_planes[:, k // PACK, k % PACK, HALF:T],
-                in_=ln_banks[1][k // 2][:, k % 2, :],
-                func=ACT.Identity,
-                bias=beta_f[:, k // PACK, k % PACK : k % PACK + 1],
-                scale=gamma_f[:, k // PACK, k % PACK : k % PACK + 1],
-            )
         for c in range(D_PASSES):
-            regroup_ln(0, c)
+            normalise_on_vector(2, c)
         for c in range(D_PASSES):
-            quantise_ln(0, c)
-        for c in range(D_PASSES):
-            regroup_ln(1, c)
-            quantise_ln(1, c)
+            normalise_on_vector(3, c)
 
-        park = out.bitcast(BF16).rearrange("r (a w) -> (r a) w", w=T)
-        h_words = keep.tile([P, F1_PASSES, T], U32, align_bytes=64)
-        h_scales = keep.tile([P, F1_PASSES, T], U8, align_bytes=64)
+        park = out.bitcast(BF16).rearrange("r (a w) -> (r a) w", w=HALF)
+        h_words = keep.tile([P, 2, F1_PASSES, HALF], U32, align_bytes=64)
+        h_scales = keep.tile([P, 2, F1_PASSES, HALF], U8, align_bytes=64)
 
-        def parked_rows(g):
-            return park[(g % PARKED) * K_PASS : (g % PARKED + 1) * K_PASS, :]
+        def parked_rows(d):
+            return park[d * PAIR * K_PASS : (d + 1) * PAIR * K_PASS, :]
 
-        def fc1_group(g):
-            h_cols = work.tile([P, PACK, T], BF16, tag="h_cols", bufs=4, name="h_cols")
-            fc1_tag = "long" if (g < LAG and g % 2 == 1) else "short"
-            for jl in range(PACK):
-                j = g * PACK + jl
-                cols = slice(j * P, (j + 1) * P)
-                acc = psum.tile([P, T], F32, tag=fc1_tag, name="fc1_acc")
-                for c in range(D_PASSES):
-                    nc.tensor.matmul_mx(
-                        out=acc[:],
-                        lhsT=w1_words[:, c, cols].bitcast(FP8X4),
-                        lhsT_scale=w1_planes[4 * c : P, cols],
-                        rhs=ln_words[:, c, :].bitcast(FP8X4),
-                        rhs_scale=ln_scales[:, c, :],
-                        start=(c == 0),
-                        stop=(c == D_PASSES - 1),
-                    )
-                nc.scalar.activation(
-                    out=h_cols[:, jl, :],
-                    in_=acc[:],
-                    func=ACT.Gelu_apprx_tanh,
-                    bias=b1_col[:, j : j + 1],
-                    scale=1.0,
+        h_cols_of = {}
+        h_rows_of = {}
+
+        w1p_words = []
+
+        def move_words(g):
+            for c in range(D_PASSES):
+                nc.vector.tensor_copy(
+                    out=w1p_words[c][:, g * K_PASS : (g + 1) * K_PASS]
+                    .bitcast(I32)
+                    .rearrange("p (t a b) -> p a t b", t=PACK, b=4),
+                    in_=w1_words[:, c, g * K_PASS : (g + 1) * K_PASS]
+                    .bitcast(I32)
+                    .rearrange("p (a b t) -> p a t b", b=4, t=PACK),
                 )
-            nc.sync.dma_start(out=parked_rows(g).rearrange("(jl m) w -> m jl w", m=P), in_=h_cols[:])
 
-        def fetch_group(g):
-            h_rows = work.tile([P, PACK, T], BF16, tag="h_rows", bufs=LAG + 1, name="h_rows")
-            nc.sync.dma_start(out=h_rows[:], in_=parked_rows(g).rearrange("(q t) w -> q t w", t=PACK))
-            return h_rows
-
-        def quantise_group(g, h_rows):
-            h_grouped = work.tile([P, T, PACK], BF16, tag="h_grouped", bufs=2, align_bytes=64, name="h_grouped")
-            nc.vector.tensor_copy(
-                out=h_grouped[:].rearrange("p (a b) t -> p a t b", b=4),
-                in_=h_rows[:].rearrange("p t (a b) -> p a t b", b=4),
-            )
-            nc.vector.quantize_mx(
-                out=h_words[:, g, :].bitcast(FP8X4),
-                scales=h_scales[:, g, :],
-                in_=h_grouped[:].rearrange("p w t -> p (w t)"),
-            )
-
-        def fc2_pass(g, i, j, acc):
-            toks = slice(i * P, (i + 1) * P)
-            cols = slice(j * N_TILE, (j + 1) * N_TILE)
+        def fc1_passes(half, j, c, acc):
+            toks = slice(half * HALF, (half + 1) * HALF)
+            cols = slice(j * P, (j + 1) * P)
             nc.tensor.matmul_mx(
                 out=acc[:],
-                lhsT=h_words[:, g, toks].bitcast(FP8X4),
-                lhsT_scale=h_scales[:, g, toks],
+                lhsT=(w1_words[:, c, cols] if half == 0 else w1p_words[c][:, cols]).bitcast(FP8X4),
+                lhsT_scale=(w1_planes if half == 0 else w1p_planes)[4 * c : P, cols],
+                rhs=ln_words[:, c, toks].bitcast(FP8X4),
+                rhs_scale=ln_scales[:, c, toks],
+                start=(c == 0),
+                stop=(c == D_PASSES - 1),
+            )
+
+        def fc1_group(half, g, by_pass):
+            if g % PAIR == 0:
+                h_cols_of[half] = work.tile(
+                    [P, PAIR * PACK, HALF], BF16, tag=("h_cols" if half == 0 else "h_stay"), bufs=(3 if half == 0 else PAIRS), name="h_cols"
+                )
+            h_cols = h_cols_of[half]
+            accs = [psum.tile([P, HALF], F32, tag="short", name="fc1_acc") for jl in range(PACK)]
+            if by_pass:
+                for c in range(D_PASSES):
+                    for jl in range(PACK):
+                        fc1_passes(half, g * PACK + jl, c, accs[jl])
+            for jl in range(PACK):
+                j = g * PACK + jl
+                if not by_pass:
+                    for c in range(D_PASSES):
+                        fc1_passes(half, j, c, accs[jl])
+                nc.scalar.activation(
+                    out=h_cols[:, (g % PAIR) * PACK + jl, :],
+                    in_=accs[jl][:],
+                    func=ACT.Gelu_apprx_tanh,
+                    bias=(b1_col[:, j : j + 1] if half == 0 else b1p[:, g, jl : jl + 1]),
+                    scale=1.0,
+                )
+            if g % PAIR == PAIR - 1:
+                if half == 0:
+                    nc.sync.dma_start(out=parked_rows(g // PAIR).rearrange("(j m) w -> m j w", m=P), in_=h_cols[:])
+                else:
+                    h_rows_of[(half, g // PAIR)] = h_cols[:].rearrange("p (e t) w -> p e (t w)", e=PAIR)
+
+        def fetch_pair(half, d):
+            h_rows = work.tile([P, PAIR, PACK * HALF], BF16, tag="h_rows", bufs=PAIRS, name="h_rows")
+            nc.sync.dma_start(
+                out=h_rows[:], in_=parked_rows(d).rearrange("(e q t) w -> q e (t w)", e=PAIR, t=PACK)
+            )
+            h_rows_of[(half, d)] = h_rows[:]
+
+        h_grouped_of = {}
+
+        def regroup_pair(half, d):
+            h_grouped = work.tile([P, PAIR, HALF, PACK], BF16, tag="h_grouped", bufs=2, align_bytes=64, name="h_grouped")
+            for e in range(PAIR):
+                nc.vector.tensor_copy(
+                    out=h_grouped[:, e, :, :].rearrange("p (a b) t -> p a t b", b=4),
+                    in_=h_rows_of[(half, d)][:, e, :].rearrange("p (t a b) -> p a t b", t=PACK, b=4),
+                )
+            h_grouped_of[(half, d)] = h_grouped
+
+        def quantise_pair(half, d):
+            h_grouped = h_grouped_of[(half, d)]
+            groups = slice(d * PAIR, (d + 1) * PAIR)
+            nc.vector.quantize_mx(
+                out=h_words[:, half, groups, :].rearrange("p g w -> p (g w)").bitcast(FP8X4),
+                scales=h_scales[:, half, groups, :].rearrange("p g w -> p (g w)"),
+                in_=h_grouped[:].rearrange("p e w t -> p (e w t)"),
+            )
+
+        def fc2_pass(g, half, b, accs):
+            toks = slice((b // F2_TILES) * P, (b // F2_TILES + 1) * P)
+            cols = slice((b % F2_TILES) * N_TILE, (b % F2_TILES + 1) * N_TILE)
+            nc.tensor.matmul_mx(
+                out=accs[b][:],
+                lhsT=h_words[:, half, g, toks].bitcast(FP8X4),
+                lhsT_scale=h_scales[:, half, g, toks],
                 rhs=w2_words[:, g, cols].bitcast(FP8X4),
                 rhs_scale=w2_planes[4 * (g % 4) : P, g // 4, cols],
                 start=(g == 0),
                 stop=(g == F1_PASSES - 1),
             )
 
-        def finish_bank(i, j, acc):
-            cols = slice(j * N_TILE, (j + 1) * N_TILE)
+        def finish_bank(half, b, accs):
+            rows = slice(half * HALF + (b // F2_TILES) * P, half * HALF + (b // F2_TILES + 1) * P)
+            cols = slice((b % F2_TILES) * N_TILE, (b % F2_TILES + 1) * N_TILE)
             res = work.tile([P, N_TILE], F32, tag="res", bufs=4, name="res")
-            nc.vector.tensor_tensor(out=res[:], in0=acc[:], in1=b2_bc[:, cols], op=ALU.add)
-            nc.sync.dma_start(out=out[i * P : (i + 1) * P, cols], in_=res[:])
+            nc.vector.tensor_tensor(out=res[:], in0=accs[b][:], in1=b2_bc[:, cols], op=ALU.add)
+            nc.sync.dma_start(out=out[rows, cols], in_=res[:])
 
-        h_rows_of = {}
-        accs0 = []
-        accs1 = []
-        for s in range(F1_PASSES + LAG):
-            if s < F1_PASSES:
-                fc1_group(s)
-            if 0 < s <= F1_PASSES:
-                h_rows_of[s - 1] = fetch_group(s - 1)
-            if W2_AHEAD + s < F1_PASSES:
-                load_w2(W2_AHEAD + s)
-            if s == F1_PASSES:
-                nc.sync.dma_start(out=b2_bc[:], in_=fc2_bias.partition_broadcast(P))
-                accs1.extend(
-                    psum.tile([P, N_TILE], F32, tag="short", name="fc2_acc1_%d" % i) for i in range(TOK_TILES)
-                )
-            if s >= F1_PASSES:
-                for i in range(TOK_TILES):
-                    fc2_pass(s - F1_PASSES, i, 1, accs1[i])
-            if s == LAG:
-                accs0.extend(
-                    psum.tile([P, N_TILE], F32, tag="long", name="fc2_acc0_%d" % i) for i in range(TOK_TILES)
-                )
-            if s >= LAG:
-                quantise_group(s - LAG, h_rows_of[s - LAG])
-                for i in range(TOK_TILES):
-                    fc2_pass(s - LAG, i, 0, accs0[i])
-        for i in range(TOK_TILES):
-            finish_bank(i, 0, accs0[i])
-        for i in range(TOK_TILES):
-            for g in range(LAG, F1_PASSES):
-                fc2_pass(g, i, 1, accs1[i])
-            finish_bank(i, 1, accs1[i])
+        BANKS = HALF_TILES * F2_TILES
+
+        for g in range(F1_PASSES):
+            fc1_group(0, g, g == 0)
+            if g % PAIR == PAIR - 1:
+                if g // PAIR > 0:
+                    fetch_pair(0, g // PAIR - 1)
+                for w in PHASE1_LOADS[g // PAIR]:
+                    load_w2(w)
+            if g == TURN_AFTER:
+                ln_banks1 = [
+                    psum.tile([P, 2, HALF], F32, tag="long", name="ln_bank1_%d" % b) for b in range(PLANES // 2)
+                ]
+                for i in (2, 3):
+                    for c in range(D_PASSES):
+                        turn(i, c, ln_banks1)
+                for k in range(PLANES):
+                    leave_on_vector(1, k, ln_banks1)
+                regroup_ln(1, 0)
+                regroup_ln(1, 1)
+                quantise_ln(1, 0)
+                quantise_ln(1, 1)
+
+        fetch_pair(0, PAIRS - 1)
+        load_w2(F1_PASSES - 2)
+        load_w2(F1_PASSES - 1)
+        nc.sync.dma_start(out=b2_bc[:], in_=fc2_bias.partition_broadcast(P))
+        w1p_words.extend(
+            work.tile([P, F1], U32, tag="big", bufs=2, align_bytes=64, name="w1p_words%d" % c) for c in range(D_PASSES)
+        )
+        for g in range(4):
+            move_words(g)
+        regroup_pair(0, 0)
+        move_words(4)
+        move_words(5)
+        quantise_pair(0, 0)
+        move_words(6)
+        move_words(7)
+        for d in range(1, PAIRS):
+            regroup_pair(0, d)
+            quantise_pair(0, d)
+        accs0 = [psum.tile([P, N_TILE], F32, tag="long", name="fc2_acc0_%d" % b) for b in range(BANKS)]
+        for g in range(F1_PASSES):
+            fc1_group(1, g, False)
+            if g in WOVEN:
+                for b in range(BANKS):
+                    fc2_pass(WOVEN[g], 0, b, accs0)
+
+        for g in range(len(WOVEN), G_MAJOR):
+            for b in range(BANKS):
+                fc2_pass(g, 0, b, accs0)
+        for d in range(2):
+            regroup_pair(1, d)
+            quantise_pair(1, d)
+        for b in range(BANKS):
+            for g in range(G_MAJOR, F1_PASSES):
+                fc2_pass(g, 0, b, accs0)
+            finish_bank(0, b, accs0)
+            if b % 2 == 1:
+                regroup_pair(1, 2 + b // 2)
+                quantise_pair(1, 2 + b // 2)
+
+        accs1 = [psum.tile([P, N_TILE], F32, tag="short", name="fc2_acc1_%d" % b) for b in range(BANKS)]
+        for g in range(G_MAJOR):
+            for b in range(BANKS):
+                fc2_pass(g, 1, b, accs1)
+        for b in range(BANKS):
+            for g in range(G_MAJOR, F1_PASSES):
+                fc2_pass(g, 1, b, accs1)
+            finish_bank(1, b, accs1)

@@ -33,8 +33,9 @@ PAIRS = F1_PASSES // PAIR
 W2_AHEAD = 1
 TURN_AFTER = 3
 PHASE1_LOADS = ((1,), (2, 3), (4,), (5,))
+SPINS = 4
 G_MAJOR = 4
-WOVEN = {3: 0, 4: 1, 6: 2}
+WOVEN = {4: 0, 5: 1, 6: 2}
 
 FLOPS = 2 * T * D * F1 + 2 * T * F1 * F2
 
@@ -68,13 +69,18 @@ def tile_layernormmlp_kernel(
         nc.vector.memset(b1_rows[:], 0.0)
         minus_half = keep.tile([P, 1], F32)
         nc.vector.memset(minus_half[:], -0.5)
+        eps = keep.tile([P, 1], F32)
+        nc.vector.memset(eps[:], EPS)
         nc.vector.memset(w2_planes[:].rearrange("p a n -> p (a n)").bitcast(I32), 0)
         ident = keep.tile([P, P], F32)
         make_identity(nc, ident[:])
 
         x_sb = keep.tile([P, TOK_TILES, D], BF16)
         for i in range(TOK_TILES):
-            nc.sync.dma_start(out=x_sb[:, i, :], in_=inputs[i * P : (i + 1) * P, :])
+            pieces = 2 if i < HALF_TILES else 1
+            for piece in range(pieces):
+                cols = slice(piece * (D // pieces), (piece + 1) * (D // pieces))
+                nc.sync.dma_start(out=x_sb[:, i, cols], in_=inputs[i * P : (i + 1) * P, cols])
 
         gamma_bf = keep.tile([P, D_PASSES, PACK], BF16)
         beta_bf = keep.tile([P, D_PASSES, PACK], BF16)
@@ -82,7 +88,7 @@ def tile_layernormmlp_kernel(
         nc.scalar.dma_start(out=gamma_bf[:], in_=gamma.rearrange("(c p t) -> p c t", p=P, t=PACK))
         nc.scalar.dma_start(out=beta_bf[:], in_=beta.rearrange("(c p t) -> p c t", p=P, t=PACK))
         warm = keep.tile([P, 1], F32)
-        nc.scalar.activation(out=warm[:], in_=zero_col[:], func=ACT.Gelu_apprx_tanh, bias=0.0, scale=1.0)
+        nc.scalar.activation(out=warm[:], in_=zero_col[:], func=ACT.Sqrt, bias=0.0, scale=1.0)
 
         for quad in range(4):
             nc.sync.dma_start(
@@ -121,6 +127,7 @@ def tile_layernormmlp_kernel(
         stats = keep.tile([P, TOK_TILES, 2, 6], F32)
         mean_var = keep.tile([P, TOK_TILES, 2], F32)
         var_eps = keep.tile([P, TOK_TILES], F32)
+        std = keep.tile([P, HALF_TILES], F32)
         rstd = keep.tile([P, TOK_TILES], F32)
         shift = keep.tile([P, TOK_TILES], F32)
         xhat = work.tile([P, TOK_TILES, D_PASSES, PACK, P], F32, tag="big", bufs=2, align_bytes=64, name="xhat")
@@ -142,12 +149,20 @@ def tile_layernormmlp_kernel(
             nc.vector.bn_aggr(
                 out=mean_var[:, i, :], in_=stats[:, i, :, :].rearrange("p h s -> p (h s)")
             )
+            if i < HALF_TILES:
+                nc.scalar.activation(
+                    out=std[:, i : i + 1], in_=mean_var[:, i, 1:2], func=ACT.Sqrt, bias=eps[:, 0:1], scale=1.0
+                )
+                return
             nc.vector.tensor_scalar(
                 out=var_eps[:, i : i + 1], in0=mean_var[:, i, 1:2], scalar1=EPS, scalar2=None, op0=ALU.add
             )
             nc.gpsimd.tensor_tensor(
                 out=rstd[:, i : i + 1], in0=var_eps[:, i : i + 1], in1=minus_half[:], op=ALU.pow
             )
+
+        def inverse_of(i):
+            nc.vector.reciprocal(out=rstd[:, i : i + 1], in_=std[:, i : i + 1])
 
         def shift_of(i):
             nc.vector.scalar_tensor_tensor(
@@ -223,30 +238,37 @@ def tile_layernormmlp_kernel(
         nc.gpsimd.tensor_copy(out=gamma_f[:], in_=gamma_bf[:])
         nc.gpsimd.tensor_copy(out=beta_f[:], in_=beta_bf[:])
         first_statistics(1)
+        inverse_of(0)
         shift_of(0)
-        last_statistics(1)
         b1_bank = psum.tile([P, P], F32, tag="short", name="b1_bank")
         nc.tensor.transpose(b1_bank[:], b1_rows_f[:], ident[:])
         ln_banks0 = [psum.tile([P, 2, HALF], F32, tag="short", name="ln_bank0_%d" % b) for b in range(PLANES // 2)]
-        for c in range(D_PASSES):
-            normalise_on_scalar(0, c)
-            turn(0, c, ln_banks0)
+        normalise_on_scalar(0, 0)
+        turn(0, 0, ln_banks0)
+        last_statistics(1)
+        normalise_on_scalar(0, 1)
+        turn(0, 1, ln_banks0)
+        inverse_of(1)
         nc.scalar.activation(out=b1_col[:], in_=b1_bank[:, 0:F1_TILES], func=ACT.Identity, bias=0.0, scale=1.0)
         nc.scalar.dma_start(out=b1p[:], in_=fc1_bias.rearrange("(g p t) -> p g t", p=P, t=PACK))
-        first_statistics(2)
         for c in range(D_PASSES):
             normalise_on_vector(1, c)
             turn(1, c, ln_banks0)
+        spin = psum.tile([P, N_TILE], F32, tag="long", name="spin")
+        for n in range(SPINS):
+            nc.tensor.matmul(out=spin[:], lhsT=b1_rows[:], rhs=x_sb[:, 0, 0:N_TILE], start=True, stop=True)
         leave_on_scalar(0, 0, ln_banks0)
         leave_on_scalar(0, 1, ln_banks0)
         leave_on_vector(0, 2, ln_banks0)
         leave_on_vector(0, 3, ln_banks0)
         for k in range(PACK, PLANES):
             leave_on_scalar(0, k, ln_banks0)
+        nc.scalar.activation(out=warm[:], in_=zero_col[:], func=ACT.Gelu_apprx_tanh, bias=0.0, scale=1.0)
         regroup_ln(0, 0)
         quantise_ln(0, 0)
         regroup_ln(0, 1)
         quantise_ln(0, 1)
+        first_statistics(2)
         last_statistics(2)
         first_statistics(3)
         last_statistics(3)
@@ -343,6 +365,15 @@ def tile_layernormmlp_kernel(
                 )
             h_grouped_of[(half, d)] = h_grouped
 
+        def regroup_pair_on_scalar(half, d):
+            h_grouped = work.tile([P, PAIR, HALF, PACK], BF16, tag="h_grouped_s", bufs=2, align_bytes=64, name="h_grouped_s")
+            for e in range(PAIR):
+                nc.scalar.copy(
+                    out=h_grouped[:, e, :, :].rearrange("p (a b) t -> p a t b", b=4),
+                    in_=h_rows_of[(half, d)][:, e, :].rearrange("p (t a b) -> p a t b", t=PACK, b=4),
+                )
+            h_grouped_of[(half, d)] = h_grouped
+
         def quantise_pair(half, d):
             h_grouped = h_grouped_of[(half, d)]
             groups = slice(d * PAIR, (d + 1) * PAIR)
@@ -352,11 +383,11 @@ def tile_layernormmlp_kernel(
                 in_=h_grouped[:].rearrange("p e w t -> p (e w t)"),
             )
 
-        def fc2_pass(g, half, b, accs):
+        def fc2_pass(g, half, b, acc, first=0, width=N_TILE):
             toks = slice((b // F2_TILES) * P, (b // F2_TILES + 1) * P)
-            cols = slice((b % F2_TILES) * N_TILE, (b % F2_TILES + 1) * N_TILE)
+            cols = slice((b % F2_TILES) * N_TILE + first, (b % F2_TILES) * N_TILE + first + width)
             nc.tensor.matmul_mx(
-                out=accs[b][:],
+                out=acc[:, 0:width],
                 lhsT=h_words[:, half, g, toks].bitcast(FP8X4),
                 lhsT_scale=h_scales[:, half, g, toks],
                 rhs=w2_words[:, g, cols].bitcast(FP8X4),
@@ -365,12 +396,14 @@ def tile_layernormmlp_kernel(
                 stop=(g == F1_PASSES - 1),
             )
 
-        def finish_bank(half, b, accs):
+        def finish_bank(half, b, acc, first=0, width=N_TILE):
             rows = slice(half * HALF + (b // F2_TILES) * P, half * HALF + (b // F2_TILES + 1) * P)
-            cols = slice((b % F2_TILES) * N_TILE, (b % F2_TILES + 1) * N_TILE)
+            cols = slice((b % F2_TILES) * N_TILE + first, (b % F2_TILES) * N_TILE + first + width)
             res = work.tile([P, N_TILE], F32, tag="res", bufs=4, name="res")
-            nc.vector.tensor_tensor(out=res[:], in0=accs[b][:], in1=b2_bc[:, cols], op=ALU.add)
-            nc.sync.dma_start(out=out[rows, cols], in_=res[:])
+            nc.vector.tensor_tensor(
+                out=res[:, 0:width], in0=acc[:, 0:width], in1=b2_bc[:, cols], op=ALU.add
+            )
+            nc.sync.dma_start(out=out[rows, cols], in_=res[:, 0:width])
 
         BANKS = HALF_TILES * F2_TILES
 
@@ -402,15 +435,9 @@ def tile_layernormmlp_kernel(
         w1p_words.extend(
             work.tile([P, F1], U32, tag="big", bufs=2, align_bytes=64, name="w1p_words%d" % c) for c in range(D_PASSES)
         )
-        for g in range(4):
+        for g in range(F1_PASSES):
             move_words(g)
-        regroup_pair(0, 0)
-        move_words(4)
-        move_words(5)
-        quantise_pair(0, 0)
-        move_words(6)
-        move_words(7)
-        for d in range(1, PAIRS):
+        for d in range(PAIRS):
             regroup_pair(0, d)
             quantise_pair(0, d)
         accs0 = [psum.tile([P, N_TILE], F32, tag="long", name="fc2_acc0_%d" % b) for b in range(BANKS)]
@@ -418,27 +445,34 @@ def tile_layernormmlp_kernel(
             fc1_group(1, g, False)
             if g in WOVEN:
                 for b in range(BANKS):
-                    fc2_pass(WOVEN[g], 0, b, accs0)
+                    fc2_pass(WOVEN[g], 0, b, accs0[b])
+
+        for d in range(2, PAIRS):
+            regroup_pair_on_scalar(1, d)
 
         for g in range(len(WOVEN), G_MAJOR):
             for b in range(BANKS):
-                fc2_pass(g, 0, b, accs0)
+                fc2_pass(g, 0, b, accs0[b])
         for d in range(2):
             regroup_pair(1, d)
             quantise_pair(1, d)
+        for d in range(2, PAIRS):
+            quantise_pair(1, d)
         for b in range(BANKS):
             for g in range(G_MAJOR, F1_PASSES):
-                fc2_pass(g, 0, b, accs0)
-            finish_bank(0, b, accs0)
-            if b % 2 == 1:
-                regroup_pair(1, 2 + b // 2)
-                quantise_pair(1, 2 + b // 2)
+                fc2_pass(g, 0, b, accs0[b])
+            finish_bank(0, b, accs0[b])
 
-        accs1 = [psum.tile([P, N_TILE], F32, tag="short", name="fc2_acc1_%d" % b) for b in range(BANKS)]
+        accs1 = [psum.tile([P, N_TILE], F32, tag="short", name="fc2_acc1_%d" % b) for b in range(BANKS - 1)]
         for g in range(G_MAJOR):
-            for b in range(BANKS):
-                fc2_pass(g, 1, b, accs1)
-        for b in range(BANKS):
+            for b in range(BANKS - 1):
+                fc2_pass(g, 1, b, accs1[b])
+        for b in range(BANKS - 1):
             for g in range(G_MAJOR, F1_PASSES):
-                fc2_pass(g, 1, b, accs1)
-            finish_bank(1, b, accs1)
+                fc2_pass(g, 1, b, accs1[b])
+            finish_bank(1, b, accs1[b])
+        for part in range(2):
+            acc = psum.tile([P, N_TILE // 2], F32, tag=("short" if part == 0 else "long"), name="fc2_acc1_last")
+            for g in range(F1_PASSES):
+                fc2_pass(g, 1, BANKS - 1, acc, part * (N_TILE // 2), N_TILE // 2)
+            finish_bank(1, BANKS - 1, acc, part * (N_TILE // 2), N_TILE // 2)

@@ -33,6 +33,7 @@ PAIRS = F1_PASSES // PAIR
 W2_AHEAD = 1
 TURN_AFTER = 3
 PHASE1_LOADS = ((1,), (2, 3), (4,), (5,))
+EARLY_SPINS = 8
 SPINS = 4
 G_MAJOR = 4
 WOVEN = {4: 0, 5: 1, 6: 2}
@@ -241,6 +242,9 @@ def tile_layernormmlp_kernel(
         inverse_of(0)
         shift_of(0)
         b1_bank = psum.tile([P, P], F32, tag="short", name="b1_bank")
+        spin = psum.tile([P, N_TILE], F32, tag="long", name="spin")
+        for n in range(EARLY_SPINS):
+            nc.tensor.matmul(out=spin[:], lhsT=x_sb[:, 0, 0:P], rhs=x_sb[:, 0, 0:N_TILE], start=True, stop=True)
         nc.tensor.transpose(b1_bank[:], b1_rows_f[:], ident[:])
         ln_banks0 = [psum.tile([P, 2, HALF], F32, tag="short", name="ln_bank0_%d" % b) for b in range(PLANES // 2)]
         normalise_on_scalar(0, 0)
@@ -254,9 +258,8 @@ def tile_layernormmlp_kernel(
         for c in range(D_PASSES):
             normalise_on_vector(1, c)
             turn(1, c, ln_banks0)
-        spin = psum.tile([P, N_TILE], F32, tag="long", name="spin")
         for n in range(SPINS):
-            nc.tensor.matmul(out=spin[:], lhsT=b1_rows[:], rhs=x_sb[:, 0, 0:N_TILE], start=True, stop=True)
+            nc.tensor.matmul(out=spin[:], lhsT=x_sb[:, 0, 0:P], rhs=x_sb[:, 0, 0:N_TILE], start=True, stop=True)
         leave_on_scalar(0, 0, ln_banks0)
         leave_on_scalar(0, 1, ln_banks0)
         leave_on_vector(0, 2, ln_banks0)

@@ -35,6 +35,7 @@ TURN_AFTER = 3
 PHASE1_LOADS = ((1,), (2, 3), (4,), (5,))
 EARLY_SPINS = 8
 SPINS = 4
+LONG_GROUPS = ((0, 1), (0, 6), (1, 0), (1, 2))
 G_MAJOR = 4
 WOVEN = {4: 0, 5: 1, 6: 2}
 
@@ -327,7 +328,8 @@ def tile_layernormmlp_kernel(
                     [P, PAIR * PACK, HALF], BF16, tag=("h_cols" if half == 0 else "h_stay"), bufs=(3 if half == 0 else PAIRS), name="h_cols"
                 )
             h_cols = h_cols_of[half]
-            accs = [psum.tile([P, HALF], F32, tag="short", name="fc1_acc") for jl in range(PACK)]
+            tag = "long" if (half, g) in LONG_GROUPS else "short"
+            accs = [psum.tile([P, HALF], F32, tag=tag, name="fc1_acc") for jl in range(PACK)]
             if by_pass:
                 for c in range(D_PASSES):
                     for jl in range(PACK):
@@ -443,9 +445,11 @@ def tile_layernormmlp_kernel(
         for d in range(PAIRS):
             regroup_pair(0, d)
             quantise_pair(0, d)
-        accs0 = [psum.tile([P, N_TILE], F32, tag="long", name="fc2_acc0_%d" % b) for b in range(BANKS)]
+        accs0 = []
         for g in range(F1_PASSES):
             fc1_group(1, g, False)
+            if g in WOVEN and WOVEN[g] == 0:
+                accs0.extend(psum.tile([P, N_TILE], F32, tag="long", name="fc2_acc0_%d" % b) for b in range(BANKS))
             if g in WOVEN:
                 for b in range(BANKS):
                     fc2_pass(WOVEN[g], 0, b, accs0[b])

from contextlib import ExitStack

import concourse.mybir as mybir
from concourse.masks import make_identity

F32 = mybir.dt.float32
BF16 = mybir.dt.bfloat16
I32 = mybir.dt.int32
U32 = mybir.dt.uint32
U8 = mybir.dt.uint8
FP8X4 = mybir.dt.float8_e4m3fn_x4
ALU = mybir.AluOpType
ACT = mybir.ActivationFunctionType

P = 128
PACK = 4
K_PASS = P * PACK
N_TILE = 512

T, D, F1, F2 = 512, 1024, 4096, 1024
EPS = 1e-3
TOK_TILES = T // P
HALF = T // 2
HALF_TILES = HALF // P
D_PASSES = D // K_PASS
PLANES = D_PASSES * PACK
F1_PASSES = F1 // K_PASS
F1_TILES = F1 // P
F2_TILES = F2 // N_TILE
W1_CHUNK = 1024
PAIR = 2
PAIRS = F1_PASSES // PAIR
W2_AHEAD = 1
TURN_AFTER = 3
PHASE1_LOADS = ((1,), (2, 3), (4,), (5,))
EARLY_SPINS = 8
SPINS = 4
LONG_GROUPS = ((0, 1), (0, 6), (1, 0), (1, 2))
G_MAJOR = 4
WOVEN = {4: 0, 5: 1, 6: 2}

FLOPS = 2 * T * D * F1 + 2 * T * F1 * F2


def tile_layernormmlp_kernel(
    tc,
    inputs,
    gamma,
    beta,
    fc1_kernel_words,
    fc1_kernel_scales,
    fc1_bias,
    fc2_kernel_words,
    fc2_kernel_scales,
    fc2_bias,
    out,
):
    nc = tc.nc
    with ExitStack() as ctx:
        keep = ctx.enter_context(tc.tile_pool(name="keep", bufs=1))
        work = ctx.enter_context(tc.tile_pool(name="work", bufs=1))
        psum = ctx.enter_context(tc.psum_pool(name="psum", bufs=4))
        ctx.enter_context(tc.manual_schedule())

        zero_col = keep.tile([P, 1], F32)
        nc.vector.memset(zero_col[:], 0.0)
        w1_planes = keep.tile([P, F1], U8, align_bytes=64)
        w2_planes = keep.tile([P, F1_PASSES // 4, F2], U8, align_bytes=64)
        nc.vector.memset(w1_planes[:].bitcast(I32), 0)
        b1_rows = keep.tile([P, P], BF16)
        nc.vector.memset(b1_rows[:], 0.0)
        minus_half = keep.tile([P, 1], F32)
        nc.vector.memset(minus_half[:], -0.5)
        eps = keep.tile([P, 1], F32)
        nc.vector.memset(eps[:], EPS)
        nc.vector.memset(w2_planes[:].rearrange("p a n -> p (a n)").bitcast(I32), 0)
        ident = keep.tile([P, P], F32)
        make_identity(nc, ident[:])

        x_sb = keep.tile([P, TOK_TILES, D], BF16)
        for i in range(TOK_TILES):
            pieces = 2 if i < HALF_TILES else 1
            for piece in range(pieces):
                cols = slice(piece * (D // pieces), (piece + 1) * (D // pieces))
                nc.sync.dma_start(out=x_sb[:, i, cols], in_=inputs[i * P : (i + 1) * P, cols])

        gamma_bf = keep.tile([P, D_PASSES, PACK], BF16)
        beta_bf = keep.tile([P, D_PASSES, PACK], BF16)
        nc.scalar.dma_start(out=b1_rows[0:F1_TILES, :], in_=fc1_bias.rearrange("(j m) -> j m", m=P))
        nc.scalar.dma_start(out=gamma_bf[:], in_=gamma.rearrange("(c p t) -> p c t", p=P, t=PACK))
        nc.scalar.dma_start(out=beta_bf[:], in_=beta.rearrange("(c p t) -> p c t", p=P, t=PACK))
        warm = keep.tile([P, 1], F32)
        nc.scalar.activation(out=warm[:], in_=zero_col[:], func=ACT.Sqrt, bias=0.0, scale=1.0)

        for quad in range(4):
            nc.sync.dma_start(
                out=w1_planes[32 * quad : 32 * quad + 4 * D_PASSES, :].bitcast(I32),
                in_=fc1_kernel_scales[:, 4 * quad : 4 * quad + 4, :].bitcast(I32),
            )
        w1p_planes = keep.tile([P, F1], U8, align_bytes=64)
        w1_words = keep.tile([P, D_PASSES, F1], U32, align_bytes=64)
        for chunk in range(F1 // W1_CHUNK):
            cols = slice(chunk * W1_CHUNK, (chunk + 1) * W1_CHUNK)
            byte_cols = slice(chunk * W1_CHUNK * PACK, (chunk + 1) * W1_CHUNK * PACK)
            for c in range(D_PASSES):
                nc.sync.dma_start(
                    out=w1_words[:, c, cols].bitcast(I32),
                    in_=fc1_kernel_words[c].rearrange("p n t -> p (n t)")[:, byte_cols].bitcast(I32),
                )

        for four in range(F1_PASSES // 4):
            for quad in range(4):
                nc.sync.dma_start(
                    out=w2_planes[32 * quad : 32 * quad + 16, four, :].bitcast(I32),
                    in_=fc2_kernel_scales[4 * four : 4 * four + 4, 4 * quad : 4 * quad + 4, :].bitcast(I32),
                )
        w2_words = keep.tile([P, F1_PASSES, F2], U32, align_bytes=64)

        def load_w2(g):
            nc.sync.dma_start(
                out=w2_words[:, g, :].bitcast(I32),
                in_=fc2_kernel_words[g].rearrange("p n t -> p (n t)").bitcast(I32),
            )

        for g in range(W2_AHEAD):
            load_w2(g)
        b2_bc = keep.tile([P, F2], BF16)

        stats = keep.tile([P, TOK_TILES, 2, 6], F32)
        mean_var = keep.tile([P, TOK_TILES, 2], F32)
        var_eps = keep.tile([P, TOK_TILES], F32)
        std = keep.tile([P, HALF_TILES], F32)
        rstd = keep.tile([P, TOK_TILES], F32)
        shift = keep.tile([P, TOK_TILES], F32)
        xhat = work.tile([P, TOK_TILES, D_PASSES, PACK, P], F32, tag="big", bufs=2, align_bytes=64, name="xhat")
        b1p = keep.tile([P, F1_PASSES, PACK], BF16)
        gamma_f = keep.tile([P, D_PASSES, PACK], F32)
        beta_f = keep.tile([P, D_PASSES, PACK], F32)
        b1_rows_f = keep.tile([P, P], F32)
        b1_col = keep.tile([P, F1_TILES], F32)
        ln_planes = keep.tile([P, D_PASSES, PACK, T], BF16)
        ln_grouped = keep.tile([P, D_PASSES, T, PACK], BF16, align_bytes=64)
        ln_words = keep.tile([P, D_PASSES, T], U32, align_bytes=64)
        ln_scales = keep.tile([P, D_PASSES, T], U8, align_bytes=64)

        def first_statistics(i):
            nc.vector.bn_stats(out=stats[:, i, 0, :], in_=x_sb[:, i, 0:512])

        def last_statistics(i):
            nc.vector.bn_stats(out=stats[:, i, 1, :], in_=x_sb[:, i, 512:1024])
            nc.vector.bn_aggr(
                out=mean_var[:, i, :], in_=stats[:, i, :, :].rearrange("p h s -> p (h s)")
            )
            if i < HALF_TILES:
                nc.scalar.activation(
                    out=std[:, i : i + 1], in_=mean_var[:, i, 1:2], func=ACT.Sqrt, bias=eps[:, 0:1], scale=1.0
                )
                return
            nc.vector.tensor_scalar(
                out=var_eps[:, i : i + 1], in0=mean_var[:, i, 1:2], scalar1=EPS, scalar2=None, op0=ALU.add
            )
            nc.gpsimd.tensor_tensor(
                out=rstd[:, i : i + 1], in0=var_eps[:, i : i + 1], in1=minus_half[:], op=ALU.pow
            )

        def inverse_of(i):
            nc.vector.reciprocal(out=rstd[:, i : i + 1], in_=std[:, i : i + 1])

        def shift_of(i):
            nc.vector.scalar_tensor_tensor(
                out=shift[:, i : i + 1],
                in0=mean_var[:, i, 0:1],
                scalar=-1.0,
                in1=rstd[:, i : i + 1],
                op0=ALU.mult,
                op1=ALU.mult,
            )

        def normalise_on_scalar(i, c):
            nc.scalar.activation(
                out=xhat[:, i, c, :, :].rearrange("p t q -> p q t"),
                in_=x_sb[:, i, c * K_PASS : (c + 1) * K_PASS].rearrange("p (q t) -> p q t", t=PACK),
                func=ACT.Identity,
                bias=shift[:, i : i + 1],
                scale=rstd[:, i : i + 1],
            )

        def normalise_on_vector(i, c):
            nc.vector.tensor_scalar(
                out=xhat[:, i, c, :, :].rearrange("p t q -> p q t"),
                in0=x_sb[:, i, c * K_PASS : (c + 1) * K_PASS].rearrange("p (q t) -> p q t", t=PACK),
                scalar1=mean_var[:, i, 0:1],
                scalar2=rstd[:, i : i + 1],
                op0=ALU.subtract,
                op1=ALU.mult,
            )

        def turn(i, c, banks):
            toks = slice((i % HALF_TILES) * P, (i % HALF_TILES + 1) * P)
            for k in range(c * PACK, (c + 1) * PACK):
                nc.tensor.transpose(banks[k // 2][:, k % 2, toks], xhat[:, i, k // PACK, k % PACK, :], ident[:])

        def leave_on_vector(half, k, banks):
            nc.vector.tensor_scalar(
                out=ln_planes[:, k // PACK, k % PACK, half * HALF : (half + 1) * HALF],
                in0=banks[k // 2][:, k % 2, :],
                scalar1=gamma_f[:, k // PACK, k % PACK : k % PACK + 1],
                scalar2=beta_f[:, k // PACK, k % PACK : k % PACK + 1],
                op0=ALU.mult,
                op1=ALU.add,
            )

        def leave_on_scalar(half, k, banks):
            nc.scalar.activation(
                out=ln_planes[:, k // PACK, k % PACK, half * HALF : (half + 1) * HALF],
                in_=banks[k // 2][:, k % 2, :],
                func=ACT.Identity,
                bias=beta_f[:, k // PACK, k % PACK : k % PACK + 1],
                scale=gamma_f[:, k // PACK, k % PACK : k % PACK + 1],
            )

        def regroup_ln(half, c):
            toks = slice(half * HALF, (half + 1) * HALF)
            nc.vector.tensor_copy(
                out=ln_grouped[:, c, toks, :].rearrange("p (a b) t -> p a t b", b=4),
                in_=ln_planes[:, c, :, toks].rearrange("p t (a b) -> p a t b", b=4),
            )

        def quantise_ln(half, c):
            toks = slice(half * HALF, (half + 1) * HALF)
            nc.vector.quantize_mx(
                out=ln_words[:, c, toks].bitcast(FP8X4),
                scales=ln_scales[:, c, toks],
                in_=ln_grouped[:, c, toks, :].rearrange("p w t -> p (w t)"),
            )

        first_statistics(0)
        last_statistics(0)
        nc.gpsimd.tensor_copy(out=b1_rows_f[:], in_=b1_rows[:])
        nc.gpsimd.tensor_copy(out=gamma_f[:], in_=gamma_bf[:])
        nc.gpsimd.tensor_copy(out=beta_f[:], in_=beta_bf[:])
        first_statistics(1)
        inverse_of(0)
        shift_of(0)
        b1_bank = psum.tile([P, P], F32, tag="short", name="b1_bank")
        spin = psum.tile([P, N_TILE], F32, tag="long", name="spin")
        for n in range(EARLY_SPINS):
            nc.tensor.matmul(out=spin[:], lhsT=x_sb[:, 0, 0:P], rhs=x_sb[:, 0, 0:N_TILE], start=True, stop=True)
        nc.tensor.transpose(b1_bank[:], b1_rows_f[:], ident[:])
        ln_banks0 = [psum.tile([P, 2, HALF], F32, tag="short", name="ln_bank0_%d" % b) for b in range(PLANES // 2)]
        normalise_on_scalar(0, 0)
        turn(0, 0, ln_banks0)
        last_statistics(1)
        normalise_on_scalar(0, 1)
        turn(0, 1, ln_banks0)
        inverse_of(1)
        nc.scalar.activation(out=b1_col[:], in_=b1_bank[:, 0:F1_TILES], func=ACT.Identity, bias=0.0, scale=1.0)
        nc.scalar.dma_start(out=b1p[:], in_=fc1_bias.rearrange("(g p t) -> p g t", p=P, t=PACK))
        for c in range(D_PASSES):
            normalise_on_vector(1, c)
            turn(1, c, ln_banks0)
        for n in range(SPINS):
            nc.tensor.matmul(out=spin[:], lhsT=x_sb[:, 0, 0:P], rhs=x_sb[:, 0, 0:N_TILE], start=True, stop=True)
        leave_on_scalar(0, 0, ln_banks0)
        leave_on_scalar(0, 1, ln_banks0)
        leave_on_vector(0, 2, ln_banks0)
        leave_on_vector(0, 3, ln_banks0)
        for k in range(PACK, PLANES):
            leave_on_scalar(0, k, ln_banks0)
        nc.scalar.activation(out=warm[:], in_=zero_col[:], func=ACT.Gelu_apprx_tanh, bias=0.0, scale=1.0)
        regroup_ln(0, 0)
        quantise_ln(0, 0)
        regroup_ln(0, 1)
        quantise_ln(0, 1)
        first_statistics(2)
        last_statistics(2)
        first_statistics(3)
        last_statistics(3)
        for t in range(PACK):
            nc.gpsimd.tensor_copy(
                out=w1p_planes[:].rearrange("p (g t m) -> p t g m", t=PACK, m=P)[:, t, :, :],
                in_=w1_planes[:].rearrange("p (g m t) -> p t g m", m=P, t=PACK)[:, t, :, :],
            )
        for c in range(D_PASSES):
            normalise_on_vector(2, c)
        for c in range(D_PASSES):
            normalise_on_vector(3, c)

        park = out.bitcast(BF16).rearrange("r (a w) -> (r a) w", w=HALF)
        h_words = keep.tile([P, 2, F1_PASSES, HALF], U32, align_bytes=64)
        h_scales = keep.tile([P, 2, F1_PASSES, HALF], U8, align_bytes=64)

        def parked_rows(d):
            return park[d * PAIR * K_PASS : (d + 1) * PAIR * K_PASS, :]

        h_cols_of = {}
        h_rows_of = {}

        w1p_words = []

        def move_words(g):
            for c in range(D_PASSES):
                nc.vector.tensor_copy(
                    out=w1p_words[c][:, g * K_PASS : (g + 1) * K_PASS]
                    .bitcast(I32)
                    .rearrange("p (t a b) -> p a t b", t=PACK, b=4),
                    in_=w1_words[:, c, g * K_PASS : (g + 1) * K_PASS]
                    .bitcast(I32)
                    .rearrange("p (a b t) -> p a t b", b=4, t=PACK),
                )

        def fc1_passes(half, j, c, acc):
            toks = slice(half * HALF, (half + 1) * HALF)
            cols = slice(j * P, (j + 1) * P)
            nc.tensor.matmul_mx(
                out=acc[:],
                lhsT=(w1_words[:, c, cols] if half == 0 else w1p_words[c][:, cols]).bitcast(FP8X4),
                lhsT_scale=(w1_planes if half == 0 else w1p_planes)[4 * c : P, cols],
                rhs=ln_words[:, c, toks].bitcast(FP8X4),
                rhs_scale=ln_scales[:, c, toks],
                start=(c == 0),
                stop=(c == D_PASSES - 1),
            )

        def fc1_group(half, g, by_pass):
            if g % PAIR == 0:
                h_cols_of[half] = work.tile(
                    [P, PAIR * PACK, HALF], BF16, tag=("h_cols" if half == 0 else "h_stay"), bufs=(3 if half == 0 else PAIRS), name="h_cols"
                )
            h_cols = h_cols_of[half]
            tag = "long" if (half, g) in LONG_GROUPS else "short"
            accs = [psum.tile([P, HALF], F32, tag=tag, name="fc1_acc") for jl in range(PACK)]
            if by_pass:
                for c in range(D_PASSES):
                    for jl in range(PACK):
                        fc1_passes(half, g * PACK + jl, c, accs[jl])
            for jl in range(PACK):
                j = g * PACK + jl
                if not by_pass:
                    for c in range(D_PASSES):
                        fc1_passes(half, j, c, accs[jl])
                nc.scalar.activation(
                    out=h_cols[:, (g % PAIR) * PACK + jl, :],
                    in_=accs[jl][:],
                    func=ACT.Gelu_apprx_tanh,
                    bias=(b1_col[:, j : j + 1] if half == 0 else b1p[:, g, jl : jl + 1]),
                    scale=1.0,
                )
            if g % PAIR == PAIR - 1:
                if half == 0:
                    nc.sync.dma_start(out=parked_rows(g // PAIR).rearrange("(j m) w -> m j w", m=P), in_=h_cols[:])
                else:
                    h_rows_of[(half, g // PAIR)] = h_cols[:].rearrange("p (e t) w -> p e (t w)", e=PAIR)

        def fetch_pair(half, d):
            h_rows = work.tile([P, PAIR, PACK * HALF], BF16, tag="h_rows", bufs=PAIRS, name="h_rows")
            nc.sync.dma_start(
                out=h_rows[:], in_=parked_rows(d).rearrange("(e q t) w -> q e (t w)", e=PAIR, t=PACK)
            )
            h_rows_of[(half, d)] = h_rows[:]

        h_grouped_of = {}

        def regroup_pair(half, d):
            h_grouped = work.tile([P, PAIR, HALF, PACK], BF16, tag="h_grouped", bufs=2, align_bytes=64, name="h_grouped")
            for e in range(PAIR):
                nc.vector.tensor_copy(
                    out=h_grouped[:, e, :, :].rearrange("p (a b) t -> p a t b", b=4),
                    in_=h_rows_of[(half, d)][:, e, :].rearrange("p (t a b) -> p a t b", t=PACK, b=4),
                )
            h_grouped_of[(half, d)] = h_grouped

        def regroup_pair_on_scalar(half, d):
            h_grouped = work.tile([P, PAIR, HALF, PACK], BF16, tag="h_grouped_s", bufs=2, align_bytes=64, name="h_grouped_s")
            for e in range(PAIR):
                nc.scalar.copy(
                    out=h_grouped[:, e, :, :].rearrange("p (a b) t -> p a t b", b=4),
                    in_=h_rows_of[(half, d)][:, e, :].rearrange("p (t a b) -> p a t b", t=PACK, b=4),
                )
            h_grouped_of[(half, d)] = h_grouped

        def quantise_pair(half, d):
            h_grouped = h_grouped_of[(half, d)]
            groups = slice(d * PAIR, (d + 1) * PAIR)
            nc.vector.quantize_mx(
                out=h_words[:, half, groups, :].rearrange("p g w -> p (g w)").bitcast(FP8X4),
                scales=h_scales[:, half, groups, :].rearrange("p g w -> p (g w)"),
                in_=h_grouped[:].rearrange("p e w t -> p (e w t)"),
            )

        def fc2_pass(g, half, b, acc, first=0, width=N_TILE):
            toks = slice((b // F2_TILES) * P, (b // F2_TILES + 1) * P)
            cols = slice((b % F2_TILES) * N_TILE + first, (b % F2_TILES) * N_TILE + first + width)
            nc.tensor.matmul_mx(
                out=acc[:, 0:width],
                lhsT=h_words[:, half, g, toks].bitcast(FP8X4),
                lhsT_scale=h_scales[:, half, g, toks],
                rhs=w2_words[:, g, cols].bitcast(FP8X4),
                rhs_scale=w2_planes[4 * (g % 4) : P, g // 4, cols],
                start=(g == 0),
                stop=(g == F1_PASSES - 1),
            )

        def finish_bank(half, b, acc, first=0, width=N_TILE):
            rows = slice(half * HALF + (b // F2_TILES) * P, half * HALF + (b // F2_TILES + 1) * P)
            cols = slice((b % F2_TILES) * N_TILE + first, (b % F2_TILES) * N_TILE + first + width)
            res = work.tile([P, N_TILE], F32, tag="res", bufs=4, name="res")
            nc.vector.tensor_tensor(
                out=res[:, 0:width], in0=acc[:, 0:width], in1=b2_bc[:, cols], op=ALU.add
            )
            nc.sync.dma_start(out=out[rows, cols], in_=res[:, 0:width])

        BANKS = HALF_TILES * F2_TILES

        for g in range(F1_PASSES):
            fc1_group(0, g, g == 0)
            if g % PAIR == PAIR - 1:
                if g // PAIR > 0:
                    fetch_pair(0, g // PAIR - 1)
                for w in PHASE1_LOADS[g // PAIR]:
                    load_w2(w)
            if g == TURN_AFTER:
                ln_banks1 = [
                    psum.tile([P, 2, HALF], F32, tag="long", name="ln_bank1_%d" % b) for b in range(PLANES // 2)
                ]
                for i in (2, 3):
                    for c in range(D_PASSES):
                        turn(i, c, ln_banks1)
                for k in range(PLANES):
                    leave_on_vector(1, k, ln_banks1)
                regroup_ln(1, 0)
                regroup_ln(1, 1)
                quantise_ln(1, 0)
                quantise_ln(1, 1)

        fetch_pair(0, PAIRS - 1)
        load_w2(F1_PASSES - 2)
        load_w2(F1_PASSES - 1)
        nc.sync.dma_start(out=b2_bc[:], in_=fc2_bias.partition_broadcast(P))
        w1p_words.extend(
            work.tile([P, F1], U32, tag="big", bufs=2, align_bytes=64, name="w1p_words%d" % c) for c in range(D_PASSES)
        )
        for g in range(F1_PASSES):
            move_words(g)
        for d in range(PAIRS):
            regroup_pair(0, d)
            quantise_pair(0, d)
        accs0 = []
        for g in range(F1_PASSES):
            fc1_group(1, g, False)
            if g in WOVEN and WOVEN[g] == 0:
                accs0.extend(psum.tile([P, N_TILE], F32, tag="long", name="fc2_acc0_%d" % b) for b in range(BANKS))
            if g in WOVEN:
                for b in range(BANKS):
                    fc2_pass(WOVEN[g], 0, b, accs0[b])

        for d in range(2, PAIRS):
            regroup_pair_on_scalar(1, d)

        for g in range(len(WOVEN), G_MAJOR):
            for b in range(BANKS):
                fc2_pass(g, 0, b, accs0[b])
        for d in range(2):
            regroup_pair(1, d)
            quantise_pair(1, d)
        for d in range(2, PAIRS):
            quantise_pair(1, d)
        for b in range(BANKS):
            for g in range(G_MAJOR, F1_PASSES):
                fc2_pass(g, 0, b, accs0[b])
            finish_bank(0, b, accs0[b])

        accs1 = [psum.tile([P, N_TILE], F32, tag="short", name="fc2_acc1_%d" % b) for b in range(BANKS - 1)]
        for g in range(G_MAJOR):
            for b in range(BANKS - 1):
                fc2_pass(g, 1, b, accs1[b])
        for b in range(BANKS - 1):
            for g in range(G_MAJOR, F1_PASSES):
                fc2_pass(g, 1, b, accs1[b])
            finish_bank(1, b, accs1[b])
        for part in range(2):
            acc = psum.tile([P, N_TILE // 2], F32, tag=("short" if part == 0 else "long"), name="fc2_acc1_last")
            for g in range(F1_PASSES):
                fc2_pass(g, 1, BANKS - 1, acc, part * (N_TILE // 2), N_TILE // 2)
            finish_bank(1, BANKS - 1, acc, part * (N_TILE // 2), N_TILE // 2)
